import numpy as np
import ml_dtypes


def mxq(x, axis, fmt="e4m3"):
    dtype, down = {"e4m3": (ml_dtypes.float8_e4m3fn, 7), "e5m2": (ml_dtypes.float8_e5m2, 14)}[fmt]
    v = np.moveaxis(np.asarray(x, np.float32).astype(ml_dtypes.bfloat16).astype(np.float64), axis, -1)
    blocks = v.reshape(v.shape[:-1] + (-1, 32))
    amax = np.abs(blocks).max(-1, keepdims=True)
    byte = np.maximum(np.where(amax > 0, np.frexp(amax)[1] - 1 + 127, 0) - down, 1)
    scale = np.exp2(byte - 127.0)
    codes = (blocks / scale).astype(np.float32).astype(dtype).astype(np.float64)
    return np.moveaxis((codes * scale).reshape(v.shape), -1, axis)


WIDE = False


def mx_kscale(k):
    if not WIDE:
        return np.ones(k)
    levels = np.array([10, -10, 5, -5, 0])
    a = np.random.permutation(np.resize(levels, k // 512 * 4)).reshape(k // 512, 4)
    idx = np.arange(k)
    return np.exp2(a[idx // 512, idx % 128 // 32])


BF16 = ml_dtypes.bfloat16


def bf(x):
    return np.asarray(x, np.float32).astype(BF16)


def f64(x):
    return np.asarray(x).astype(np.float64)


B, LQ, LK, D = 4, 1024, 128, 1024
EPS = 1e-8


def softmax(v):
    e = np.exp(v - v.max(-1, keepdims=True))
    return e / e.sum(-1, keepdims=True)


def setup_inputs():
    s = mx_kscale(D)
    sc = 1.0 / np.sqrt(D)
    base = np.array([0.0, 1.5, 0.5])
    return {
        "query": bf(np.random.standard_normal((B, LQ, D)) * s),
        "key": bf(np.random.standard_normal((B, LK, D)) * s),
        "Wq": bf(np.random.standard_normal((D, D)) * sc / s[None, :]),
        "bq": bf(np.random.standard_normal(D) * 0.2),
        "Wk": bf(np.random.standard_normal((D, D)) * sc / s[None, :]),
        "bk": bf(np.random.standard_normal(D) * 0.2),
        "scoring_weights": bf(base + 0.1 * np.random.standard_normal(base.shape)),
    }


def reference(query, key, Wq, bq, Wk, bk, scoring_weights):
    q = np.tanh((mxq(f64(query), 2, "e4m3") @ mxq(f64(Wq), 1, "e4m3").T) + f64(bq))
    k = np.tanh((mxq(f64(key), 2, "e4m3") @ mxq(f64(Wk), 1, "e4m3").T) + f64(bk))
    dot = mxq(q, 2, "e4m3") @ mxq(k, 2, "e4m3").transpose(0, 2, 1)
    qn = np.sqrt((q * q).sum(-1))
    kn = np.sqrt((k * k).sum(-1))
    cos = dot / np.maximum(qn[:, :, None] * kn[:, None, :], EPS)
    sq = np.maximum(qn[:, :, None] ** 2 + kn[:, None, :] ** 2 - 2.0 * dot, 0.0)
    euc = -np.sqrt(sq)
    w = softmax(f64(scoring_weights))
    scores = w[0] * dot + w[1] * cos + w[2] * euc
    return softmax(scores)

@@ -1,0 +1,344 @@
+from contextlib import ExitStack
+
+import concourse.mybir as mybir
+from concourse.masks import make_identity
+
+F32 = mybir.dt.float32
+BF16 = mybir.dt.bfloat16
+U32 = mybir.dt.uint32
+U8 = mybir.dt.uint8
+FP8X4 = mybir.dt.float8_e4m3fn_x4
+ACT = mybir.ActivationFunctionType
+ALU = mybir.AluOpType
+AX = mybir.AxisListType
+
+P = 128
+D = 1024
+B = 4
+LQ = 1024
+LK = 128
+G = 2
+FT = 8
+RB = 512
+NBLK = 9
+LEAD = 6
+EPS = 1e-8
+
+FLOPS = 2 * (B * LQ + B * LK) * D * D + 2 * B * LQ * LK * D
+
+
+def tile_adaptiveattention_pa_t_kernel(tc, query, key, Wq, bq, Wk, bk, scoring_weights, out):
+    nc = tc.nc
+    with ExitStack() as ctx:
+        ctx.enter_context(tc.manual_schedule())
+        const = ctx.enter_context(tc.tile_pool(name="const", bufs=1))
+        wpool = ctx.enter_context(tc.tile_pool(name="wpool", bufs=1))
+        xpool = ctx.enter_context(tc.tile_pool(name="xpool", bufs=2))
+        qpool = ctx.enter_context(tc.tile_pool(name="qpool", bufs=2))
+        fin = ctx.enter_context(tc.tile_pool(name="fin", bufs=1))
+        psum = ctx.enter_context(tc.psum_pool(name="psum", bufs=1))
+
+        q_blocks = query.rearrange("b (h t p) k -> (b h) p t k", h=2, t=4, p=P)
+        key_view = key.rearrange("b p k -> p b k")
+        out_blocks = out.rearrange("b (h t p) j -> (b h) p t j", h=2, t=4, p=P)
+        wk_view = Wk.rearrange("(t p) k -> p t k", p=P)
+        wq_view = Wq.rearrange("(t p) k -> p t k", p=P)
+
+        brow = const.tile([P, P], BF16, name="brow")
+        nc.vector.memset(brow[:], 0.0)
+        nc.sync.dma_start(out=brow[0:8, :], in_=bq.rearrange("(r c) -> r c", c=P))
+        nc.sync.dma_start(out=brow[8:16, :], in_=bk.rearrange("(r c) -> r c", c=P))
+        sw_b = const.tile([P, 3], BF16, name="sw_b")
+        nc.sync.dma_start(out=sw_b[:], in_=scoring_weights.partition_broadcast(P))
+
+        wk_nat = wpool.tile([P, FT, D], BF16, name="wk_nat", tag="wnat", bufs=2)
+        wq_nat = wpool.tile([P, FT, D], BF16, name="wq_nat", tag="wnat", bufs=2)
+        x_nat = {}
+
+        def load_block(i):
+            t = xpool.tile([P, 4, D], BF16, name="x_nat%d" % i, tag="x_nat", bufs=3)
+            nc.sync.dma_start(out=t[:], in_=key_view if i == 0 else q_blocks[i - 1])
+            x_nat[i] = t
+
+        nc.sync.dma_start(out=wk_nat[:, 0:4, :], in_=wk_view[:, 0:4, :])
+        nc.sync.dma_start(out=wk_nat[:, 4:8, :], in_=wk_view[:, 4:8, :])
+        load_block(0)
+        nc.sync.dma_start(out=wq_nat[:, 0:4, :], in_=wq_view[:, 0:4, :])
+        nc.sync.dma_start(out=wq_nat[:, 4:8, :], in_=wq_view[:, 4:8, :])
+        load_block(1)
+        load_block(2)
+
+        ident = const.tile([P, P], F32, name="ident")
+        make_identity(nc, ident[:])
+        neghalf = const.tile([P, 4], F32, name="neghalf")
+        nc.gpsimd.memset(neghalf[:], -0.5)
+
+        bias_f = const.tile([P, P], F32, name="bias_f")
+        nc.vector.tensor_copy(out=bias_f[:], in_=brow[:])
+        bias_ps = psum.tile([P, 4, P], F32, name="bias_ps", tag="dot")
+        nc.tensor.transpose(bias_ps[:, 0, :], bias_f[:], ident[:])
+        bias_col = const.tile([P, 16], F32, name="bias_col")
+        nc.vector.tensor_copy(out=bias_col[:], in_=bias_ps[:, 0, 0:16])
+
+        wc = const.tile([P, 8], F32, name="wc")
+        sw_f = const.tile([P, 3], F32, name="sw_f")
+        sw_m = const.tile([P, 1], F32, name="sw_m")
+        sw_s = const.tile([P, 1], F32, name="sw_s")
+        sw_r = const.tile([P, 1], F32, name="sw_r")
+        sw_e = const.tile([P, 3], F32, name="sw_e")
+        nc.vector.tensor_copy(out=sw_f[:], in_=sw_b[:])
+        nc.vector.tensor_reduce(out=sw_m[:], in_=sw_f[:], axis=AX.X, op=ALU.max, negate=True)
+        nc.scalar.activation(out=sw_e[:], in_=sw_f[:], func=ACT.Exp, bias=sw_m[:], scale=1.0, accum_out=sw_s[:])
+        nc.vector.reciprocal(out=sw_r[:], in_=sw_s[:])
+        nc.vector.tensor_scalar(out=wc[:, 0:3], in0=sw_e[:], scalar1=sw_r[:], scalar2=None, op0=ALU.mult)
+        nc.vector.tensor_tensor(out=wc[:, 3:4], in0=wc[:, 2:3], in1=wc[:, 2:3], op=ALU.mult)
+        nc.vector.tensor_scalar(out=wc[:, 4:5], in0=wc[:, 1:2], scalar1=1.0 / EPS, scalar2=None, op0=ALU.mult)
+        w0c = wc[:, 0:1]
+        w1c = wc[:, 1:2]
+        w2sq = wc[:, 3:4]
+        w1cap = wc[:, 4:5]
+
+        def words(grp):
+            return grp[:].bitcast(F32).rearrange("p (g r u) -> p g r u", g=G, u=2)
+
+        def transpose_tile(nat_row_tile, dst, tag, bufs, on_scalar):
+            ps = psum.tile([P, 4, P], F32, name="tr_ps", tag=tag, bufs=bufs)
+            src = nat_row_tile.bitcast(F32)
+            for j in range(4):
+                nc.tensor.transpose(ps[:, j, :], src[:, P * j : P * (j + 1)], ident[:])
+            view = ps[:].rearrange("p (g u) r -> p g r u", g=G)
+            if on_scalar:
+                nc.scalar.copy(out=dst, in_=view)
+            else:
+                nc.vector.tensor_copy(out=dst, in_=view)
+
+        def quantise(grp, rows, codes, scales, g, c0, c1):
+            nc.vector.quantize_mx(
+                out=codes[:, g, c0:c1].bitcast(FP8X4),
+                scales=scales[:, g, c0:c1],
+                in_=grp[:, (g * rows + c0) * 4 : (g * rows + c1) * 4],
+            )
+
+        def prepare_weights(nat, label):
+            grp = wpool.tile([P, G * D * 4], BF16, name="w_grp" + label, tag="w_grp", align_bytes=64)
+            codes = wpool.tile([P, G, D], U32, name="w_codes" + label, align_bytes=64)
+            scales = wpool.tile([P, G, D], U8, name="w_scales" + label, align_bytes=64)
+            view = words(grp)
+            for t in range(FT):
+                transpose_tile(
+                    nat[:, t, :], view[:, :, P * t : P * (t + 1), :], "nt" if t % 2 == 0 else "mm", 3, t % 2 == 1
+                )
+                if t % 4 == 3:
+                    for g in range(G):
+                        quantise(grp, D, codes, scales, g, P * (t - 3), P * (t + 1))
+            return codes, scales
+
+        x_grp = {}
+        x_codes = {}
+        x_scales = {}
+
+        def input_tile(tau, on_scalar):
+            i, rt = tau // 4, tau % 4
+            if rt == 0:
+                x_grp[i] = xpool.tile([P, G * RB * 4], BF16, name="x_grp%d" % i, tag="x_grp", align_bytes=64)
+                x_codes[i] = xpool.tile([P, G, RB], U32, name="x_codes%d" % i, tag="x_codes", align_bytes=64)
+                x_scales[i] = xpool.tile([P, G, RB], U8, name="x_scales%d" % i, tag="x_scales", align_bytes=64)
+            transpose_tile(x_nat[i][:, rt, :], words(x_grp[i])[:, :, P * rt : P * (rt + 1), :], "tr", 1, on_scalar)
+            if rt == 3:
+                for g in range(G):
+                    quantise(x_grp[i], RB, x_codes[i], x_scales[i], g, 0, RB)
+                if i + 3 < NBLK:
+                    load_block(i + 3)
+
+        wk_codes, wk_scales = prepare_weights(wk_nat, "k")
+        for tau in range(4):
+            input_tile(tau, tau % 2 == 1)
+        wq_codes, wq_scales = prepare_weights(wq_nat, "q")
+        for tau in range(4, LEAD):
+            input_tile(tau, tau % 2 == 1)
+
+        n2p = fin.tile([P, 4 * NBLK, 2], F32, name="n2p")
+        n2 = fin.tile([P, 4 * NBLK], F32, name="n2")
+        rn = fin.tile([P, 4 * NBLK], F32, name="rn")
+        rnw = fin.tile([P, 4 * NBLK], F32, name="rnw")
+        kn2_bc = fin.tile([P, B, LK], F32, name="kn2_bc")
+        rkn_bc = fin.tile([P, B, LK], F32, name="rkn_bc")
+        sq_all = fin.tile([P, 8, RB], F32, name="sq_all")
+        t_all = fin.tile([P, 8, RB], F32, name="t_all")
+        negmax = fin.tile([P, 32], F32, name="negmax")
+        esum = fin.tile([P, 32], F32, name="esum")
+        rsum = fin.tile([P, 32], F32, name="rsum")
+        k_codes = fin.tile([P, G, RB], U32, name="k_codes", align_bytes=64)
+        k_scales = fin.tile([P, G, RB], U8, name="k_scales", align_bytes=64)
+
+        qf = {}
+        q_grp = {}
+        q_codes = {0: k_codes}
+        q_scales = {0: k_scales}
+        r_cos = {}
+        n2sum = {}
+        dots = {}
+
+        def project(i, ft):
+            s = 2 * i + ft // 4
+            if ft % 4 == 0:
+                qf[s] = qpool.tile([P, 4, RB], F32, name="qf%d" % s, tag="qf", bufs=3)
+            wc_, ws_ = (wk_codes, wk_scales) if i == 0 else (wq_codes, wq_scales)
+            acc = psum.tile([P, RB], F32, name="acc", tag="mm", bufs=3)
+            for g in range(G):
+                nc.tensor.matmul_mx(
+                    out=acc[:],
+                    lhsT=wc_[:, g, P * ft : P * (ft + 1)].bitcast(FP8X4),
+                    lhsT_scale=ws_[:, g, P * ft : P * (ft + 1)],
+                    rhs=x_codes[i][:, g, :].bitcast(FP8X4),
+                    rhs_scale=x_scales[i][:, g, :],
+                    start=(g == 0),
+                    stop=(g == G - 1),
+                )
+            col = (8 if i == 0 else 0) + ft
+            nc.scalar.activation(
+                out=qf[s][:, ft % 4, :], in_=acc[:], func=ACT.Tanh, bias=bias_col[:, col : col + 1], scale=1.0
+            )
+
+        def norm_tile(s, rt):
+            i, h = s // 2, s % 2
+            pn = psum.tile([P, 4, P], F32, name="pn", tag="nt", bufs=3)
+            for t in range(4):
+                nc.tensor.transpose(pn[:, t, :], qf[s][:, t, P * rt : P * (rt + 1)], ident[:])
+            junk = qpool.tile([P, RB], BF16, name="junk", tag="junk")
+            nc.scalar.activation(
+                out=junk[:],
+                in_=pn[:].rearrange("p t f -> p (t f)"),
+                func=ACT.Square,
+                accum_out=n2p[:, 4 * i + rt, h : h + 1],
+            )
+
+        def regroup(s):
+            q_grp[s] = qpool.tile([P, RB * 4], BF16, name="q_grp%d" % s, tag="q_grp", align_bytes=64)
+            nc.vector.tensor_copy(
+                out=q_grp[s][:].rearrange("p (w t) -> p w t", t=4), in_=qf[s][:].rearrange("p t w -> p w t")
+            )
+
+        def quantise_q(s):
+            i, h = s // 2, s % 2
+            if i > 0 and h == 0:
+                q_codes[i] = qpool.tile([P, G, RB], U32, name="q_codes%d" % i, tag="q_codes", align_bytes=64)
+                q_scales[i] = qpool.tile([P, G, RB], U8, name="q_scales%d" % i, tag="q_scales", align_bytes=64)
+            nc.vector.quantize_mx(
+                out=q_codes[i][:, h, :].bitcast(FP8X4), scales=q_scales[i][:, h, :], in_=q_grp[s][:]
+            )
+
+        def norms(i):
+            c = slice(4 * i, 4 * i + 4)
+            nc.gpsimd.tensor_tensor(out=n2[:, c], in0=n2p[:, c, 0], in1=n2p[:, c, 1], op=ALU.add)
+            nc.gpsimd.tensor_tensor(out=rn[:, c], in0=n2[:, c], in1=neghalf[:], op=ALU.pow)
+            if i > 0:
+                nc.gpsimd.tensor_scalar(
+                    out=rnw[:, c], in0=rn[:, c], scalar1=w1c, scalar2=0.0, op0=ALU.mult, op1=ALU.add
+                )
+
+        def spread_key_norms():
+            for src, dst in ((n2, kn2_bc), (rn, rkn_bc)):
+                ps = psum.tile([P, 4, P], F32, name="kn_ps", tag="tr", bufs=1)
+                for b in range(B):
+                    rep = fin.tile([P, P], F32, name="rep", tag="rep", bufs=2)
+                    nc.vector.tensor_copy(out=rep[:], in_=src[:, b : b + 1].to_broadcast([P, P]))
+                    nc.tensor.transpose(ps[:, b, :], rep[:], ident[:])
+                nc.vector.tensor_copy(out=dst[:], in_=ps[:])
+
+        def pair_terms(i):
+            b = (i - 1) // 2
+            r_cos[i] = qpool.tile([P, 4, LK], F32, name="r_cos%d" % i, tag="r_cos")
+            n2sum[i] = qpool.tile([P, 4, LK], F32, name="n2sum%d" % i, tag="n2sum")
+            for rt in range(4):
+                c = 4 * i + rt
+                nc.gpsimd.tensor_scalar(
+                    out=r_cos[i][:, rt, :], in0=rkn_bc[:, b, :], scalar1=rnw[:, c : c + 1], scalar2=w1cap,
+                    op0=ALU.mult, op1=ALU.min,
+                )
+                nc.gpsimd.tensor_scalar(
+                    out=n2sum[i][:, rt, :], in0=kn2_bc[:, b, :], scalar1=1.0, scalar2=n2[:, c : c + 1],
+                    op0=ALU.mult, op1=ALU.add,
+                )
+
+        def dot(i):
+            b = (i - 1) // 2
+            pd = psum.tile([P, 4, LK], F32, name="pd", tag="dot")
+            for rt in range(4):
+                for g in range(G):
+                    nc.tensor.matmul_mx(
+                        out=pd[:, rt, :],
+                        lhsT=q_codes[i][:, g, P * rt : P * (rt + 1)].bitcast(FP8X4),
+                        lhsT_scale=q_scales[i][:, g, P * rt : P * (rt + 1)],
+                        rhs=k_codes[:, g, LK * b : LK * (b + 1)].bitcast(FP8X4),
+                        rhs_scale=k_scales[:, g, LK * b : LK * (b + 1)],
+                        start=(g == 0),
+                        stop=(g == G - 1),
+                    )
+            dots[i] = pd
+
+        def mix(i):
+            d = dots[i][:].rearrange("p t j -> p (t j)")
+            nc.vector.scalar_tensor_tensor(
+                out=sq_all[:, i - 1, :], in0=d, scalar=-2.0, in1=n2sum[i][:].rearrange("p t j -> p (t j)"),
+                op0=ALU.mult, op1=ALU.add,
+            )
+            nc.vector.scalar_tensor_tensor(
+                out=t_all[:, i - 1, :], in0=r_cos[i][:].rearrange("p t j -> p (t j)"), scalar=w0c, in1=d,
+                op0=ALU.add, op1=ALU.mult,
+            )
+            nc.gpsimd.tensor_scalar(
+                out=sq_all[:, i - 1, :], in0=sq_all[:, i - 1, :], scalar1=0.0, scalar2=w2sq,
+                op0=ALU.max, op1=ALU.mult,
+            )
+
+        n_phase = 4 * NBLK
+        for ph in range(n_phase + 6):
+            s, c = ph // 2, ph % 2
+            i = ph // 4
+            if ph < n_phase:
+                ft = 2 * (ph % 4)
+                project(i, ft)
+                project(i, ft + 1)
+            if ph % 4 == 3 and 1 <= (ph - 7) // 4 <= 8:
+                dot((ph - 7) // 4)
+            if 1 <= s <= 2 * NBLK:
+                norm_tile(s - 1, 2 * c)
+                norm_tile(s - 1, 2 * c + 1)
+            if ph + LEAD < n_phase:
+                input_tile(ph + LEAD, False)
+            if 1 <= s <= 2 * NBLK:
+                if c == 0:
+                    regroup(s - 1)
+                else:
+                    quantise_q(s - 1)
+            if ph % 4 == 2 and ph >= 6:
+                j = (ph - 6) // 4
+                norms(j)
+                if j > 0:
+                    pair_terms(j)
+            if ph == 8:
+                spread_key_norms()
+            if ph % 4 == 1 and 1 <= (ph - 9) // 4 <= 8:
+                mix((ph - 9) // 4)
+
+        for r in range(8):
+            nc.scalar.activation(out=sq_all[:, r, :], in_=sq_all[:, r, :], func=ACT.Sqrt)
+            nc.vector.tensor_tensor(out=t_all[:, r, :], in0=t_all[:, r, :], in1=sq_all[:, r, :], op=ALU.subtract)
+            nc.vector.tensor_reduce(
+                out=negmax[:, 4 * r : 4 * r + 4], in_=t_all[:, r, :].rearrange("p (t j) -> p t j", t=4),
+                axis=AX.X, op=ALU.max, negate=True,
+            )
+        for r in range(8):
+            for rt in range(4):
+                c = 4 * r + rt
+                nc.scalar.activation(
+                    out=sq_all[:, r, LK * rt : LK * (rt + 1)], in_=t_all[:, r, LK * rt : LK * (rt + 1)],
+                    func=ACT.Exp, bias=negmax[:, c : c + 1], scale=1.0, accum_out=esum[:, c : c + 1],
+                )
+            nc.vector.reciprocal(out=rsum[:, 4 * r : 4 * r + 4], in_=esum[:, 4 * r : 4 * r + 4])
+            e3 = sq_all[:, r, :].rearrange("p (t j) -> p t j", t=4)
+            nc.vector.tensor_tensor(
+                out=e3, in0=e3, in1=rsum[:, 4 * r : 4 * r + 4].unsqueeze(2).to_broadcast([P, 4, LK]), op=ALU.mult
+            )
+            nc.sync.dma_start(out=out_blocks[r], in_=e3)

@@ -21,6 +21,7 @@ G = 2
 FT = 8
 RB = 512
 NBLK = 9
+RING = 7
 LEAD = 6
 EPS = 1e-8
 
@@ -101,8 +102,8 @@ def tile_adaptiveattention_pa_t_kernel(tc, query, key, Wq, bq, Wk, bk, scoring_w
         def words(grp):
             return grp[:].bitcast(F32).rearrange("p (g r u) -> p g r u", g=G, u=2)
 
-        def transpose_tile(nat_row_tile, dst, tag, bufs, on_scalar):
-            ps = psum.tile([P, 4, P], F32, name="tr_ps", tag=tag, bufs=bufs)
+        def transpose_tile(nat_row_tile, dst, on_scalar):
+            ps = psum.tile([P, 4, P], F32, name="tr_ps", tag="ring", bufs=RING)
             src = nat_row_tile.bitcast(F32)
             for j in range(4):
                 nc.tensor.transpose(ps[:, j, :], src[:, P * j : P * (j + 1)], ident[:])
@@ -125,9 +126,7 @@ def tile_adaptiveattention_pa_t_kernel(tc, query, key, Wq, bq, Wk, bk, scoring_w
             scales = wpool.tile([P, G, D], U8, name="w_scales" + label, align_bytes=64)
             view = words(grp)
             for t in range(FT):
-                transpose_tile(
-                    nat[:, t, :], view[:, :, P * t : P * (t + 1), :], "nt" if t % 2 == 0 else "mm", 3, t % 2 == 1
-                )
+                transpose_tile(nat[:, t, :], view[:, :, P * t : P * (t + 1), :], t % 2 == 1)
                 if t % 4 == 3:
                     for g in range(G):
                         quantise(grp, D, codes, scales, g, P * (t - 3), P * (t + 1))
@@ -143,7 +142,7 @@ def tile_adaptiveattention_pa_t_kernel(tc, query, key, Wq, bq, Wk, bk, scoring_w
                 x_grp[i] = xpool.tile([P, G * RB * 4], BF16, name="x_grp%d" % i, tag="x_grp", align_bytes=64)
                 x_codes[i] = xpool.tile([P, G, RB], U32, name="x_codes%d" % i, tag="x_codes", align_bytes=64)
                 x_scales[i] = xpool.tile([P, G, RB], U8, name="x_scales%d" % i, tag="x_scales", align_bytes=64)
-            transpose_tile(x_nat[i][:, rt, :], words(x_grp[i])[:, :, P * rt : P * (rt + 1), :], "tr", 1, on_scalar)
+            transpose_tile(x_nat[i][:, rt, :], words(x_grp[i])[:, :, P * rt : P * (rt + 1), :], on_scalar)
             if rt == 3:
                 for g in range(G):
                     quantise(x_grp[i], RB, x_codes[i], x_scales[i], g, 0, RB)
@@ -176,7 +175,6 @@ def tile_adaptiveattention_pa_t_kernel(tc, query, key, Wq, bq, Wk, bk, scoring_w
         q_codes = {0: k_codes}
         q_scales = {0: k_scales}
         r_cos = {}
-        n2sum = {}
         dots = {}
 
         def project(i, ft):
@@ -184,7 +182,7 @@ def tile_adaptiveattention_pa_t_kernel(tc, query, key, Wq, bq, Wk, bk, scoring_w
             if ft % 4 == 0:
                 qf[s] = qpool.tile([P, 4, RB], F32, name="qf%d" % s, tag="qf", bufs=3)
             wc_, ws_ = (wk_codes, wk_scales) if i == 0 else (wq_codes, wq_scales)
-            acc = psum.tile([P, RB], F32, name="acc", tag="mm", bufs=3)
+            acc = psum.tile([P, RB], F32, name="acc", tag="ring", bufs=RING)
             for g in range(G):
                 nc.tensor.matmul_mx(
                     out=acc[:],
@@ -202,7 +200,7 @@ def tile_adaptiveattention_pa_t_kernel(tc, query, key, Wq, bq, Wk, bk, scoring_w
 
         def norm_tile(s, rt):
             i, h = s // 2, s % 2
-            pn = psum.tile([P, 4, P], F32, name="pn", tag="nt", bufs=3)
+            pn = psum.tile([P, 4, P], F32, name="pn", tag="ring", bufs=RING)
             for t in range(4):
                 nc.tensor.transpose(pn[:, t, :], qf[s][:, t, P * rt : P * (rt + 1)], ident[:])
             junk = qpool.tile([P, RB], BF16, name="junk", tag="junk")
@@ -239,7 +237,7 @@ def tile_adaptiveattention_pa_t_kernel(tc, query, key, Wq, bq, Wk, bk, scoring_w
 
         def spread_key_norms():
             for src, dst in ((n2, kn2_bc), (rn, rkn_bc)):
-                ps = psum.tile([P, 4, P], F32, name="kn_ps", tag="tr", bufs=1)
+                ps = psum.tile([P, 4, P], F32, name="kn_ps", tag="ring", bufs=RING)
                 for b in range(B):
                     rep = fin.tile([P, P], F32, name="rep", tag="rep", bufs=2)
                     nc.vector.tensor_copy(out=rep[:], in_=src[:, b : b + 1].to_broadcast([P, P]))
@@ -249,16 +247,11 @@ def tile_adaptiveattention_pa_t_kernel(tc, query, key, Wq, bq, Wk, bk, scoring_w
         def pair_terms(i):
             b = (i - 1) // 2
             r_cos[i] = qpool.tile([P, 4, LK], F32, name="r_cos%d" % i, tag="r_cos")
-            n2sum[i] = qpool.tile([P, 4, LK], F32, name="n2sum%d" % i, tag="n2sum")
             for rt in range(4):
                 c = 4 * i + rt
-                nc.gpsimd.tensor_scalar(
+                nc.vector.tensor_scalar(
                     out=r_cos[i][:, rt, :], in0=rkn_bc[:, b, :], scalar1=rnw[:, c : c + 1], scalar2=w1cap,
                     op0=ALU.mult, op1=ALU.min,
-                )
-                nc.gpsimd.tensor_scalar(
-                    out=n2sum[i][:, rt, :], in0=kn2_bc[:, b, :], scalar1=1.0, scalar2=n2[:, c : c + 1],
-                    op0=ALU.mult, op1=ALU.add,
                 )
 
         def dot(i):
@@ -278,19 +271,22 @@ def tile_adaptiveattention_pa_t_kernel(tc, query, key, Wq, bq, Wk, bk, scoring_w
             dots[i] = pd
 
         def mix(i):
+            b = (i - 1) // 2
             d = dots[i][:].rearrange("p t j -> p (t j)")
             nc.vector.scalar_tensor_tensor(
-                out=sq_all[:, i - 1, :], in0=d, scalar=-2.0, in1=n2sum[i][:].rearrange("p t j -> p (t j)"),
-                op0=ALU.mult, op1=ALU.add,
+                out=sq_all[:, i - 1, :].rearrange("p (t j) -> p t j", t=4), in0=dots[i][:], scalar=-2.0,
+                in1=kn2_bc[:, b : b + 1, :].to_broadcast([P, 4, LK]), op0=ALU.mult, op1=ALU.add,
             )
             nc.vector.scalar_tensor_tensor(
                 out=t_all[:, i - 1, :], in0=r_cos[i][:].rearrange("p t j -> p (t j)"), scalar=w0c, in1=d,
                 op0=ALU.add, op1=ALU.mult,
             )
-            nc.gpsimd.tensor_scalar(
-                out=sq_all[:, i - 1, :], in0=sq_all[:, i - 1, :], scalar1=0.0, scalar2=w2sq,
-                op0=ALU.max, op1=ALU.mult,
-            )
+            for rt in range(4):
+                c = 4 * i + rt
+                part = sq_all[:, i - 1, LK * rt : LK * (rt + 1)]
+                nc.vector.tensor_scalar(
+                    out=part, in0=part, scalar1=n2[:, c : c + 1], scalar2=0.0, op0=ALU.add, op1=ALU.max
+                )
 
         n_phase = 4 * NBLK
         for ph in range(n_phase + 6):
@@ -315,15 +311,15 @@ def tile_adaptiveattention_pa_t_kernel(tc, query, key, Wq, bq, Wk, bk, scoring_w
             if ph % 4 == 2 and ph >= 6:
                 j = (ph - 6) // 4
                 norms(j)
-                if j > 0:
-                    pair_terms(j)
+            if ph % 4 == 3 and 1 <= (ph - 7) // 4 <= 8:
+                pair_terms((ph - 7) // 4)
             if ph == 8:
                 spread_key_norms()
             if ph % 4 == 1 and 1 <= (ph - 9) // 4 <= 8:
                 mix((ph - 9) // 4)
 
         for r in range(8):
-            nc.scalar.activation(out=sq_all[:, r, :], in_=sq_all[:, r, :], func=ACT.Sqrt)
+            nc.scalar.activation(out=sq_all[:, r, :], in_=sq_all[:, r, :], func=ACT.Sqrt, scale=w2sq)
             nc.vector.tensor_tensor(out=t_all[:, r, :], in0=t_all[:, r, :], in1=sq_all[:, r, :], op=ALU.subtract)
             nc.vector.tensor_reduce(
                 out=negmax[:, 4 * r : 4 * r + 4], in_=t_all[:, r, :].rearrange("p (t j) -> p t j", t=4),

@@ -120,17 +120,27 @@ def tile_adaptiveattention_pa_t_kernel(tc, query, key, Wq, bq, Wk, bk, scoring_w
                 in_=grp[:, (g * rows + c0) * 4 : (g * rows + c1) * 4],
             )
 
-        def prepare_weights(nat, label):
+        def prepare_weights_after(first, nat, label):
+            return prepare_weights(nat, label, first)
+
+        def prepare_weights(nat, label, first=None):
             grp = wpool.tile([P, G * D * 4], BF16, name="w_grp" + label, tag="w_grp", align_bytes=64)
             codes = wpool.tile([P, G, D], U32, name="w_codes" + label, align_bytes=64)
             scales = wpool.tile([P, G, D], U8, name="w_scales" + label, align_bytes=64)
             view = words(grp)
             for t in range(FT):
                 transpose_tile(nat[:, t, :], view[:, :, P * t : P * (t + 1), :], t % 2 == 1)
-                if t % 4 == 3:
+                if t == 0 and first is not None:
+                    first(0)
+                if t == 4:
                     for g in range(G):
-                        quantise(grp, D, codes, scales, g, P * (t - 3), P * (t + 1))
-            return codes, scales
+                        quantise(grp, D, codes, scales, g, 0, 4 * P)
+
+            def second_half():
+                for g in range(G):
+                    quantise(grp, D, codes, scales, g, 4 * P, 8 * P)
+
+            return codes, scales, second_half
 
         x_grp = {}
         x_codes = {}
@@ -143,17 +153,22 @@ def tile_adaptiveattention_pa_t_kernel(tc, query, key, Wq, bq, Wk, bk, scoring_w
                 x_codes[i] = xpool.tile([P, G, RB], U32, name="x_codes%d" % i, tag="x_codes", align_bytes=64)
                 x_scales[i] = xpool.tile([P, G, RB], U8, name="x_scales%d" % i, tag="x_scales", align_bytes=64)
             transpose_tile(x_nat[i][:, rt, :], words(x_grp[i])[:, :, P * rt : P * (rt + 1), :], on_scalar)
-            if rt == 3:
-                for g in range(G):
-                    quantise(x_grp[i], RB, x_codes[i], x_scales[i], g, 0, RB)
-                if i + 3 < NBLK:
-                    load_block(i + 3)
+            if rt == 3 and i + 3 < NBLK:
+                load_block(i + 3)
 
-        wk_codes, wk_scales = prepare_weights(wk_nat, "k")
-        for tau in range(4):
+        def quantise_x(i):
+            for g in range(G):
+                quantise(x_grp[i], RB, x_codes[i], x_scales[i], g, 0, RB)
+
+        wk_codes, wk_scales, wk_rest = prepare_weights(wk_nat, "k")
+        input_tile(0, False)
+        wk_rest()
+        for tau in range(1, 4):
             input_tile(tau, tau % 2 == 1)
-        wq_codes, wq_scales = prepare_weights(wq_nat, "q")
-        for tau in range(4, LEAD):
+        wq_codes, wq_scales, wq_rest = prepare_weights_after(quantise_x, wq_nat, "q")
+        input_tile(4, False)
+        wq_rest()
+        for tau in range(5, LEAD):
             input_tile(tau, tau % 2 == 1)
 
         n2p = fin.tile([P, 4 * NBLK, 2], F32, name="n2p")
@@ -214,7 +229,8 @@ def tile_adaptiveattention_pa_t_kernel(tc, query, key, Wq, bq, Wk, bk, scoring_w
         def regroup(s):
             q_grp[s] = qpool.tile([P, RB * 4], BF16, name="q_grp%d" % s, tag="q_grp", align_bytes=64)
             nc.vector.tensor_copy(
-                out=q_grp[s][:].rearrange("p (w t) -> p w t", t=4), in_=qf[s][:].rearrange("p t w -> p w t")
+                out=q_grp[s][:].rearrange("p (c i t) -> p c t i", i=4, t=4),
+                in_=qf[s][:].rearrange("p t (c i) -> p c t i", i=4),
             )
 
         def quantise_q(s):
@@ -308,6 +324,8 @@ def tile_adaptiveattention_pa_t_kernel(tc, query, key, Wq, bq, Wk, bk, scoring_w
                     regroup(s - 1)
                 else:
                     quantise_q(s - 1)
+            if ph + LEAD < n_phase and (ph + LEAD) % 4 == 3:
+                quantise_x((ph + LEAD) // 4)
             if ph % 4 == 2 and ph >= 6:
                 j = (ph - 6) // 4
                 norms(j)

@@ -22,7 +22,7 @@ FT = 8
 RB = 512
 NBLK = 9
 RING = 7
-LEAD = 6
+LEAD = 8
 EPS = 1e-8
 
 FLOPS = 2 * (B * LQ + B * LK) * D * D + 2 * B * LQ * LK * D
@@ -170,6 +170,7 @@ def tile_adaptiveattention_pa_t_kernel(tc, query, key, Wq, bq, Wk, bk, scoring_w
         wq_rest()
         for tau in range(5, LEAD):
             input_tile(tau, tau % 2 == 1)
+        quantise_x(1)
 
         n2p = fin.tile([P, 4 * NBLK, 2], F32, name="n2p")
         n2 = fin.tile([P, 4 * NBLK], F32, name="n2")
@@ -304,37 +305,39 @@ def tile_adaptiveattention_pa_t_kernel(tc, query, key, Wq, bq, Wk, bk, scoring_w
                     out=part, in0=part, scalar1=n2[:, c : c + 1], scalar2=0.0, op0=ALU.add, op1=ALU.max
                 )
 
-        n_phase = 4 * NBLK
-        for ph in range(n_phase + 6):
-            s, c = ph // 2, ph % 2
-            i = ph // 4
-            if ph < n_phase:
-                ft = 2 * (ph % 4)
-                project(i, ft)
-                project(i, ft + 1)
-            if ph % 4 == 3 and 1 <= (ph - 7) // 4 <= 8:
-                dot((ph - 7) // 4)
-            if 1 <= s <= 2 * NBLK:
-                norm_tile(s - 1, 2 * c)
-                norm_tile(s - 1, 2 * c + 1)
-            if ph + LEAD < n_phase:
-                input_tile(ph + LEAD, False)
-            if 1 <= s <= 2 * NBLK:
-                if c == 0:
-                    regroup(s - 1)
-                else:
-                    quantise_q(s - 1)
-            if ph + LEAD < n_phase and (ph + LEAD) % 4 == 3:
-                quantise_x((ph + LEAD) // 4)
-            if ph % 4 == 2 and ph >= 6:
-                j = (ph - 6) // 4
-                norms(j)
-            if ph % 4 == 3 and 1 <= (ph - 7) // 4 <= 8:
-                pair_terms((ph - 7) // 4)
-            if ph == 8:
+        n_step = 2 * NBLK
+        tau = LEAD
+        for s in range(n_step + 7):
+            i, h = s // 2, s % 2
+            if s < n_step:
+                for u in range(4):
+                    project(i, 4 * h + u)
+            if s % 2 == 1 and 1 <= (s - 5) // 2 <= 8:
+                dot((s - 5) // 2)
+            if 1 <= s <= n_step:
+                for rt in range(4):
+                    norm_tile(s - 1, rt)
+            full = -1
+            for u in range(2):
+                if tau < 4 * NBLK:
+                    input_tile(tau, False)
+                    if tau % 4 == 3:
+                        full = tau // 4
+                    tau += 1
+            if 1 <= s <= n_step:
+                regroup(s - 1)
+            if full >= 0:
+                quantise_x(full)
+            if 2 <= s <= n_step + 1:
+                quantise_q(s - 2)
+            if s % 2 == 1 and 0 <= (s - 3) // 2 <= 8:
+                norms((s - 3) // 2)
+            if s % 2 == 0 and 1 <= (s - 4) // 2 <= 8:
+                pair_terms((s - 4) // 2)
+            if s == 4:
                 spread_key_norms()
-            if ph % 4 == 1 and 1 <= (ph - 9) // 4 <= 8:
-                mix((ph - 9) // 4)
+            if s % 2 == 1 and 1 <= (s - 5) // 2 <= 8:
+                mix((s - 5) // 2)
 
         for r in range(8):
             nc.scalar.activation(out=sq_all[:, r, :], in_=sq_all[:, r, :], func=ACT.Sqrt, scale=w2sq)

@@ -175,7 +175,6 @@ def tile_adaptiveattention_pa_t_kernel(tc, query, key, Wq, bq, Wk, bk, scoring_w
         n2p = fin.tile([P, 4 * NBLK, 2], F32, name="n2p")
         n2 = fin.tile([P, 4 * NBLK], F32, name="n2")
         rn = fin.tile([P, 4 * NBLK], F32, name="rn")
-        rnw = fin.tile([P, 4 * NBLK], F32, name="rnw")
         kn2_bc = fin.tile([P, B, LK], F32, name="kn2_bc")
         rkn_bc = fin.tile([P, B, LK], F32, name="rkn_bc")
         sq_all = fin.tile([P, 8, RB], F32, name="sq_all")
@@ -247,19 +246,24 @@ def tile_adaptiveattention_pa_t_kernel(tc, query, key, Wq, bq, Wk, bk, scoring_w
             c = slice(4 * i, 4 * i + 4)
             nc.gpsimd.tensor_tensor(out=n2[:, c], in0=n2p[:, c, 0], in1=n2p[:, c, 1], op=ALU.add)
             nc.gpsimd.tensor_tensor(out=rn[:, c], in0=n2[:, c], in1=neghalf[:], op=ALU.pow)
-            if i > 0:
-                nc.gpsimd.tensor_scalar(
-                    out=rnw[:, c], in0=rn[:, c], scalar1=w1c, scalar2=0.0, op0=ALU.mult, op1=ALU.add
-                )
+
+        reps = {}
+
+        def repeat_key_norms():
+            for v, src in enumerate((n2, rn)):
+                reps[v] = fin.tile([P, B, P], F32, name="rep%d" % v)
+                for b in range(B):
+                    nc.vector.tensor_copy(out=reps[v][:, b, :], in_=src[:, b : b + 1].to_broadcast([P, P]))
 
         def spread_key_norms():
-            for src, dst in ((n2, kn2_bc), (rn, rkn_bc)):
+            for v in range(2):
                 ps = psum.tile([P, 4, P], F32, name="kn_ps", tag="ring", bufs=RING)
                 for b in range(B):
-                    rep = fin.tile([P, P], F32, name="rep", tag="rep", bufs=2)
-                    nc.vector.tensor_copy(out=rep[:], in_=src[:, b : b + 1].to_broadcast([P, P]))
-                    nc.tensor.transpose(ps[:, b, :], rep[:], ident[:])
-                nc.vector.tensor_copy(out=dst[:], in_=ps[:])
+                    nc.tensor.transpose(ps[:, b, :], reps[v][:, b, :], ident[:])
+                if v == 0:
+                    nc.vector.tensor_copy(out=kn2_bc[:], in_=ps[:])
+                else:
+                    nc.vector.tensor_scalar(out=rkn_bc[:], in0=ps[:], scalar1=w1c, scalar2=None, op0=ALU.mult)
 
         def pair_terms(i):
             b = (i - 1) // 2
@@ -267,7 +271,7 @@ def tile_adaptiveattention_pa_t_kernel(tc, query, key, Wq, bq, Wk, bk, scoring_w
             for rt in range(4):
                 c = 4 * i + rt
                 nc.vector.tensor_scalar(
-                    out=r_cos[i][:, rt, :], in0=rkn_bc[:, b, :], scalar1=rnw[:, c : c + 1], scalar2=w1cap,
+                    out=r_cos[i][:, rt, :], in0=rkn_bc[:, b, :], scalar1=rn[:, c : c + 1], scalar2=w1cap,
                     op0=ALU.mult, op1=ALU.min,
                 )
 
@@ -287,17 +291,20 @@ def tile_adaptiveattention_pa_t_kernel(tc, query, key, Wq, bq, Wk, bk, scoring_w
                     )
             dots[i] = pd
 
-        def mix(i):
+        def squared_distance(i):
             b = (i - 1) // 2
-            d = dots[i][:].rearrange("p t j -> p (t j)")
             nc.vector.scalar_tensor_tensor(
                 out=sq_all[:, i - 1, :].rearrange("p (t j) -> p t j", t=4), in0=dots[i][:], scalar=-2.0,
                 in1=kn2_bc[:, b : b + 1, :].to_broadcast([P, 4, LK]), op0=ALU.mult, op1=ALU.add,
             )
+
+        def dot_and_cosine(i):
             nc.vector.scalar_tensor_tensor(
-                out=t_all[:, i - 1, :], in0=r_cos[i][:].rearrange("p t j -> p (t j)"), scalar=w0c, in1=d,
-                op0=ALU.add, op1=ALU.mult,
+                out=t_all[:, i - 1, :], in0=r_cos[i][:].rearrange("p t j -> p (t j)"), scalar=w0c,
+                in1=dots[i][:].rearrange("p t j -> p (t j)"), op0=ALU.add, op1=ALU.mult,
             )
+
+        def clamp_distance(i):
             for rt in range(4):
                 c = 4 * i + rt
                 part = sq_all[:, i - 1, LK * rt : LK * (rt + 1)]
@@ -324,6 +331,8 @@ def tile_adaptiveattention_pa_t_kernel(tc, query, key, Wq, bq, Wk, bk, scoring_w
                     if tau % 4 == 3:
                         full = tau // 4
                     tau += 1
+            if s == 5:
+                spread_key_norms()
             if 1 <= s <= n_step:
                 regroup(s - 1)
             if full >= 0:
@@ -332,12 +341,20 @@ def tile_adaptiveattention_pa_t_kernel(tc, query, key, Wq, bq, Wk, bk, scoring_w
                 quantise_q(s - 2)
             if s % 2 == 1 and 0 <= (s - 3) // 2 <= 8:
                 norms((s - 3) // 2)
-            if s % 2 == 0 and 1 <= (s - 4) // 2 <= 8:
+            if s % 2 == 0 and 1 <= (s - 4) // 2 <= 7:
                 pair_terms((s - 4) // 2)
             if s == 4:
-                spread_key_norms()
+                repeat_key_norms()
             if s % 2 == 1 and 1 <= (s - 5) // 2 <= 8:
-                mix((s - 5) // 2)
+                j = (s - 5) // 2
+                squared_distance(j)
+                if j < 8:
+                    dot_and_cosine(j)
+                    clamp_distance(j)
+                else:
+                    clamp_distance(j)
+                    pair_terms(j)
+                    dot_and_cosine(j)
 
         for r in range(8):
             nc.scalar.activation(out=sq_all[:, r, :], in_=sq_all[:, r, :], func=ACT.Sqrt, scale=w2sq)

@@ -21,8 +21,10 @@ G = 2
 FT = 8
 RB = 512
 NBLK = 9
-RING = 7
-LEAD = 8
+S_RING = 5
+V_RING = 3
+W_LEAD = 5
+Q_LEAD = 3
 EPS = 1e-8
 
 FLOPS = 2 * (B * LQ + B * LK) * D * D + 2 * B * LQ * LK * D
@@ -45,28 +47,31 @@ def tile_adaptiveattention_pa_t_kernel(tc, query, key, Wq, bq, Wk, bk, scoring_w
         wk_view = Wk.rearrange("(t p) k -> p t k", p=P)
         wq_view = Wq.rearrange("(t p) k -> p t k", p=P)
 
+        wk_nat = wpool.tile([P, FT, D], BF16, name="wk_nat")
+        wq_nat = wpool.tile([P, FT, D], BF16, name="wq_nat")
+        x_nat = {}
+
+        def load_block(i):
+            t = xpool.tile([P, 4, D], BF16, name="x_nat%d" % i, tag="x_nat", bufs=3)
+            view = key_view if i == 0 else q_blocks[i - 1]
+            for c in range(0, 4, 2):
+                nc.sync.dma_start(out=t[:, c : c + 2, :], in_=view[:, c : c + 2, :])
+            x_nat[i] = t
+
+        def load_weights(nat, view):
+            for c in range(0, FT, 2):
+                nc.sync.dma_start(out=nat[:, c : c + 2, :], in_=view[:, c : c + 2, :])
+
         brow = const.tile([P, P], BF16, name="brow")
         nc.vector.memset(brow[:], 0.0)
         nc.sync.dma_start(out=brow[0:8, :], in_=bq.rearrange("(r c) -> r c", c=P))
         nc.sync.dma_start(out=brow[8:16, :], in_=bk.rearrange("(r c) -> r c", c=P))
         sw_b = const.tile([P, 3], BF16, name="sw_b")
         nc.sync.dma_start(out=sw_b[:], in_=scoring_weights.partition_broadcast(P))
-
-        wk_nat = wpool.tile([P, FT, D], BF16, name="wk_nat", tag="wnat", bufs=2)
-        wq_nat = wpool.tile([P, FT, D], BF16, name="wq_nat", tag="wnat", bufs=2)
-        x_nat = {}
-
-        def load_block(i):
-            t = xpool.tile([P, 4, D], BF16, name="x_nat%d" % i, tag="x_nat", bufs=3)
-            nc.sync.dma_start(out=t[:], in_=key_view if i == 0 else q_blocks[i - 1])
-            x_nat[i] = t
-
-        nc.sync.dma_start(out=wk_nat[:, 0:4, :], in_=wk_view[:, 0:4, :])
-        nc.sync.dma_start(out=wk_nat[:, 4:8, :], in_=wk_view[:, 4:8, :])
         load_block(0)
-        nc.sync.dma_start(out=wq_nat[:, 0:4, :], in_=wq_view[:, 0:4, :])
-        nc.sync.dma_start(out=wq_nat[:, 4:8, :], in_=wq_view[:, 4:8, :])
+        load_weights(wk_nat, wk_view)
         load_block(1)
+        load_weights(wq_nat, wq_view)
         load_block(2)
 
         ident = const.tile([P, P], F32, name="ident")
@@ -74,36 +79,11 @@ def tile_adaptiveattention_pa_t_kernel(tc, query, key, Wq, bq, Wk, bk, scoring_w
         neghalf = const.tile([P, 4], F32, name="neghalf")
         nc.gpsimd.memset(neghalf[:], -0.5)
 
-        bias_f = const.tile([P, P], F32, name="bias_f")
-        nc.vector.tensor_copy(out=bias_f[:], in_=brow[:])
-        bias_ps = psum.tile([P, 4, P], F32, name="bias_ps", tag="dot")
-        nc.tensor.transpose(bias_ps[:, 0, :], bias_f[:], ident[:])
-        bias_col = const.tile([P, 16], F32, name="bias_col")
-        nc.vector.tensor_copy(out=bias_col[:], in_=bias_ps[:, 0, 0:16])
-
-        wc = const.tile([P, 8], F32, name="wc")
-        sw_f = const.tile([P, 3], F32, name="sw_f")
-        sw_m = const.tile([P, 1], F32, name="sw_m")
-        sw_s = const.tile([P, 1], F32, name="sw_s")
-        sw_r = const.tile([P, 1], F32, name="sw_r")
-        sw_e = const.tile([P, 3], F32, name="sw_e")
-        nc.vector.tensor_copy(out=sw_f[:], in_=sw_b[:])
-        nc.vector.tensor_reduce(out=sw_m[:], in_=sw_f[:], axis=AX.X, op=ALU.max, negate=True)
-        nc.scalar.activation(out=sw_e[:], in_=sw_f[:], func=ACT.Exp, bias=sw_m[:], scale=1.0, accum_out=sw_s[:])
-        nc.vector.reciprocal(out=sw_r[:], in_=sw_s[:])
-        nc.vector.tensor_scalar(out=wc[:, 0:3], in0=sw_e[:], scalar1=sw_r[:], scalar2=None, op0=ALU.mult)
-        nc.vector.tensor_tensor(out=wc[:, 3:4], in0=wc[:, 2:3], in1=wc[:, 2:3], op=ALU.mult)
-        nc.vector.tensor_scalar(out=wc[:, 4:5], in0=wc[:, 1:2], scalar1=1.0 / EPS, scalar2=None, op0=ALU.mult)
-        w0c = wc[:, 0:1]
-        w1c = wc[:, 1:2]
-        w2sq = wc[:, 3:4]
-        w1cap = wc[:, 4:5]
-
         def words(grp):
             return grp[:].bitcast(F32).rearrange("p (g r u) -> p g r u", g=G, u=2)
 
         def transpose_tile(nat_row_tile, dst, on_scalar):
-            ps = psum.tile([P, 4, P], F32, name="tr_ps", tag="ring", bufs=RING)
+            ps = psum.tile([P, 4, P], F32, name="tr_ps", tag="s_ring" if on_scalar else "v_ring", bufs=S_RING if on_scalar else V_RING)
             src = nat_row_tile.bitcast(F32)
             for j in range(4):
                 nc.tensor.transpose(ps[:, j, :], src[:, P * j : P * (j + 1)], ident[:])
@@ -120,27 +100,27 @@ def tile_adaptiveattention_pa_t_kernel(tc, query, key, Wq, bq, Wk, bk, scoring_w
                 in_=grp[:, (g * rows + c0) * 4 : (g * rows + c1) * 4],
             )
 
-        def prepare_weights_after(first, nat, label):
-            return prepare_weights(nat, label, first)
+        w_grp = {}
+        w_codes = {}
+        w_scales = {}
+        w_nat = {"k": wk_nat, "q": wq_nat}
+        for label in ("k", "q"):
+            w_codes[label] = wpool.tile([P, G, D], U32, name="w_codes" + label, align_bytes=64)
+            w_scales[label] = wpool.tile([P, G, D], U8, name="w_scales" + label, align_bytes=64)
 
-        def prepare_weights(nat, label, first=None):
-            grp = wpool.tile([P, G * D * 4], BF16, name="w_grp" + label, tag="w_grp", align_bytes=64)
-            codes = wpool.tile([P, G, D], U32, name="w_codes" + label, align_bytes=64)
-            scales = wpool.tile([P, G, D], U8, name="w_scales" + label, align_bytes=64)
-            view = words(grp)
-            for t in range(FT):
-                transpose_tile(nat[:, t, :], view[:, :, P * t : P * (t + 1), :], t % 2 == 1)
-                if t == 0 and first is not None:
-                    first(0)
-                if t == 4:
-                    for g in range(G):
-                        quantise(grp, D, codes, scales, g, 0, 4 * P)
+        def weight_tile(m, on_scalar):
+            label, t = "kq"[m // FT], m % FT
+            w_grp[m] = wpool.tile([P, G * P * 4], BF16, name="w_grp%d" % m, tag="w_grp", bufs=6, align_bytes=64)
+            transpose_tile(w_nat[label][:, t, :], words(w_grp[m]), on_scalar)
 
-            def second_half():
-                for g in range(G):
-                    quantise(grp, D, codes, scales, g, 4 * P, 8 * P)
-
-            return codes, scales, second_half
+        def quantise_weight_tile(m):
+            label, t = "kq"[m // FT], m % FT
+            for g in range(G):
+                nc.vector.quantize_mx(
+                    out=w_codes[label][:, g, P * t : P * (t + 1)].bitcast(FP8X4),
+                    scales=w_scales[label][:, g, P * t : P * (t + 1)],
+                    in_=w_grp[m][:, g * P * 4 : (g + 1) * P * 4],
+                )
 
         x_grp = {}
         x_codes = {}
@@ -149,9 +129,9 @@ def tile_adaptiveattention_pa_t_kernel(tc, query, key, Wq, bq, Wk, bk, scoring_w
         def input_tile(tau, on_scalar):
             i, rt = tau // 4, tau % 4
             if rt == 0:
-                x_grp[i] = xpool.tile([P, G * RB * 4], BF16, name="x_grp%d" % i, tag="x_grp", align_bytes=64)
-                x_codes[i] = xpool.tile([P, G, RB], U32, name="x_codes%d" % i, tag="x_codes", align_bytes=64)
-                x_scales[i] = xpool.tile([P, G, RB], U8, name="x_scales%d" % i, tag="x_scales", align_bytes=64)
+                x_grp[i] = xpool.tile([P, G * RB * 4], BF16, name="x_grp%d" % i, tag="x_grp", bufs=3, align_bytes=64)
+                x_codes[i] = xpool.tile([P, G, RB], U32, name="x_codes%d" % i, tag="x_codes", bufs=3, align_bytes=64)
+                x_scales[i] = xpool.tile([P, G, RB], U8, name="x_scales%d" % i, tag="x_scales", bufs=3, align_bytes=64)
             transpose_tile(x_nat[i][:, rt, :], words(x_grp[i])[:, :, P * rt : P * (rt + 1), :], on_scalar)
             if rt == 3 and i + 3 < NBLK:
                 load_block(i + 3)
@@ -159,18 +139,6 @@ def tile_adaptiveattention_pa_t_kernel(tc, query, key, Wq, bq, Wk, bk, scoring_w
         def quantise_x(i):
             for g in range(G):
                 quantise(x_grp[i], RB, x_codes[i], x_scales[i], g, 0, RB)
-
-        wk_codes, wk_scales, wk_rest = prepare_weights(wk_nat, "k")
-        input_tile(0, False)
-        wk_rest()
-        for tau in range(1, 4):
-            input_tile(tau, tau % 2 == 1)
-        wq_codes, wq_scales, wq_rest = prepare_weights_after(quantise_x, wq_nat, "q")
-        input_tile(4, False)
-        wq_rest()
-        for tau in range(5, LEAD):
-            input_tile(tau, tau % 2 == 1)
-        quantise_x(1)
 
         n2p = fin.tile([P, 4 * NBLK, 2], F32, name="n2p")
         n2 = fin.tile([P, 4 * NBLK], F32, name="n2")
@@ -195,9 +163,10 @@ def tile_adaptiveattention_pa_t_kernel(tc, query, key, Wq, bq, Wk, bk, scoring_w
         def project(i, ft):
             s = 2 * i + ft // 4
             if ft % 4 == 0:
-                qf[s] = qpool.tile([P, 4, RB], F32, name="qf%d" % s, tag="qf", bufs=3)
-            wc_, ws_ = (wk_codes, wk_scales) if i == 0 else (wq_codes, wq_scales)
-            acc = psum.tile([P, RB], F32, name="acc", tag="ring", bufs=RING)
+                qf[s] = qpool.tile([P, 4, RB], F32, name="qf%d" % s, tag="qf", bufs=5)
+            label = "k" if i == 0 else "q"
+            wc_, ws_ = w_codes[label], w_scales[label]
+            acc = psum.tile([P, RB], F32, name="acc", tag="s_ring", bufs=S_RING)
             for g in range(G):
                 nc.tensor.matmul_mx(
                     out=acc[:],
@@ -215,7 +184,7 @@ def tile_adaptiveattention_pa_t_kernel(tc, query, key, Wq, bq, Wk, bk, scoring_w
 
         def norm_tile(s, rt):
             i, h = s // 2, s % 2
-            pn = psum.tile([P, 4, P], F32, name="pn", tag="ring", bufs=RING)
+            pn = psum.tile([P, 4, P], F32, name="pn", tag="s_ring", bufs=S_RING)
             for t in range(4):
                 nc.tensor.transpose(pn[:, t, :], qf[s][:, t, P * rt : P * (rt + 1)], ident[:])
             junk = qpool.tile([P, RB], BF16, name="junk", tag="junk")
@@ -247,19 +216,11 @@ def tile_adaptiveattention_pa_t_kernel(tc, query, key, Wq, bq, Wk, bk, scoring_w
             nc.gpsimd.tensor_tensor(out=n2[:, c], in0=n2p[:, c, 0], in1=n2p[:, c, 1], op=ALU.add)
             nc.gpsimd.tensor_tensor(out=rn[:, c], in0=n2[:, c], in1=neghalf[:], op=ALU.pow)
 
-        reps = {}
-
-        def repeat_key_norms():
-            for v, src in enumerate((n2, rn)):
-                reps[v] = fin.tile([P, B, P], F32, name="rep%d" % v)
-                for b in range(B):
-                    nc.vector.tensor_copy(out=reps[v][:, b, :], in_=src[:, b : b + 1].to_broadcast([P, P]))
-
         def spread_key_norms():
             for v in range(2):
-                ps = psum.tile([P, 4, P], F32, name="kn_ps", tag="ring", bufs=RING)
+                ps = psum.tile([P, 4, P], F32, name="kn_ps", tag="v_ring", bufs=V_RING)
                 for b in range(B):
-                    nc.tensor.transpose(ps[:, b, :], reps[v][:, b, :], ident[:])
+                    nc.tensor.transpose(ps[:, b, :], (n2, rn)[v][:, b : b + 1].to_broadcast([P, P]), ident[:])
                 if v == 0:
                     nc.vector.tensor_copy(out=kn2_bc[:], in_=ps[:])
                 else:
@@ -277,7 +238,7 @@ def tile_adaptiveattention_pa_t_kernel(tc, query, key, Wq, bq, Wk, bk, scoring_w
 
         def dot(i):
             b = (i - 1) // 2
-            pd = psum.tile([P, 4, LK], F32, name="pd", tag="dot")
+            pd = psum.tile([P, 4, LK], F32, name="pd", tag="v_ring", bufs=V_RING)
             for rt in range(4):
                 for g in range(G):
                     nc.tensor.matmul_mx(
@@ -312,41 +273,86 @@ def tile_adaptiveattention_pa_t_kernel(tc, query, key, Wq, bq, Wk, bk, scoring_w
                     out=part, in0=part, scalar1=n2[:, c : c + 1], scalar2=0.0, op0=ALU.add, op1=ALU.max
                 )
 
+        def row_maxima(i):
+            r = i - 1
+            nc.vector.tensor_reduce(
+                out=negmax[:, 4 * r : 4 * r + 4], in_=t_all[:, r, :].rearrange("p (t j) -> p t j", t=4),
+                axis=AX.X, op=ALU.max, negate=True,
+            )
+
         n_step = 2 * NBLK
-        tau = LEAD
-        for s in range(n_step + 7):
-            i, h = s // 2, s % 2
+        bias_f = const.tile([P, P], F32, name="bias_f")
+        nc.vector.tensor_copy(out=bias_f[:], in_=brow[:])
+        bias_ps = psum.tile([P, 4, P], F32, name="bias_ps", tag="v_ring", bufs=V_RING)
+        nc.tensor.transpose(bias_ps[:, 0, :], bias_f[:], ident[:])
+        bias_col = const.tile([P, 16], F32, name="bias_col")
+        nc.vector.tensor_copy(out=bias_col[:], in_=bias_ps[:, 0, 0:16])
+
+        for tau in range(4):
+            input_tile(tau, tau % 2 == 0)
+        for m in range(W_LEAD):
+            weight_tile(m, m % 2 == 0 and m < 4)
+            if m == 0:
+                quantise_x(0)
+        for m in range(Q_LEAD):
+            quantise_weight_tile(m)
+        tau = 4
+        for b in range(2 * n_step + 9):
+            s, hb = b // 2, b % 2
+            j = (b - 11) // 4 if b >= 15 and b % 4 == 3 else 0
             if s < n_step:
-                for u in range(4):
-                    project(i, 4 * h + u)
-            if s % 2 == 1 and 1 <= (s - 5) // 2 <= 8:
-                dot((s - 5) // 2)
-            if 1 <= s <= n_step:
-                for rt in range(4):
-                    norm_tile(s - 1, rt)
-            full = -1
-            for u in range(2):
+                for u in (2 * hb, 2 * hb + 1):
+                    project(s // 2, 4 * (s % 2) + u)
+            if j > 0:
+                dot(j)
+            if b in (3, 7):
+                quantise_x((b + 1) // 4)
+            elif b % 4 == 1 and 9 <= b <= 29:
+                quantise_x((b + 3) // 4)
+            for m in (2 * b + Q_LEAD, 2 * b + Q_LEAD + 1):
+                if m < 2 * FT:
+                    quantise_weight_tile(m)
+            for m in (2 * b + W_LEAD, 2 * b + W_LEAD + 1):
+                if m < 2 * FT:
+                    weight_tile(m, False)
+            for u in range(0 if b in (0, 3) else 2 if b in (1, 2, 6, 7, 8) else 1):
                 if tau < 4 * NBLK:
-                    input_tile(tau, False)
-                    if tau % 4 == 3:
-                        full = tau // 4
+                    input_tile(tau, tau in (5, 7))
                     tau += 1
-            if s == 5:
-                spread_key_norms()
             if 1 <= s <= n_step:
-                regroup(s - 1)
-            if full >= 0:
-                quantise_x(full)
-            if 2 <= s <= n_step + 1:
-                quantise_q(s - 2)
-            if s % 2 == 1 and 0 <= (s - 3) // 2 <= 8:
-                norms((s - 3) // 2)
-            if s % 2 == 0 and 1 <= (s - 4) // 2 <= 7:
-                pair_terms((s - 4) // 2)
-            if s == 4:
-                repeat_key_norms()
-            if s % 2 == 1 and 1 <= (s - 5) // 2 <= 8:
-                j = (s - 5) // 2
+                for rt in (2 * hb, 2 * hb + 1):
+                    norm_tile(s - 1, rt)
+            if b == 3:
+                wc = const.tile([P, 8], F32, name="wc")
+                sw_f = const.tile([P, 3], F32, name="sw_f")
+                sw_m = const.tile([P, 1], F32, name="sw_m")
+                sw_s = const.tile([P, 1], F32, name="sw_s")
+                sw_r = const.tile([P, 1], F32, name="sw_r")
+                sw_e = const.tile([P, 3], F32, name="sw_e")
+                nc.vector.tensor_copy(out=sw_f[:], in_=sw_b[:])
+                nc.vector.tensor_reduce(out=sw_m[:], in_=sw_f[:], axis=AX.X, op=ALU.max, negate=True)
+                nc.scalar.activation(out=sw_e[:], in_=sw_f[:], func=ACT.Exp, bias=sw_m[:], scale=1.0, accum_out=sw_s[:])
+                nc.vector.reciprocal(out=sw_r[:], in_=sw_s[:])
+                nc.vector.tensor_scalar(out=wc[:, 0:3], in0=sw_e[:], scalar1=sw_r[:], scalar2=None, op0=ALU.mult)
+                nc.vector.tensor_tensor(out=wc[:, 3:4], in0=wc[:, 2:3], in1=wc[:, 2:3], op=ALU.mult)
+                nc.vector.tensor_scalar(out=wc[:, 4:5], in0=wc[:, 1:2], scalar1=1.0 / EPS, scalar2=None, op0=ALU.mult)
+                w0c = wc[:, 0:1]
+                w1c = wc[:, 1:2]
+                w2sq = wc[:, 3:4]
+                w1cap = wc[:, 4:5]
+            if b == 12:
+                spread_key_norms()
+            for r in range(n_step):
+                if b == max(2 * r + 5, r + 9):
+                    quantise_q(r)
+            for r in range(n_step):
+                if b == max(2 * r + 3, r + 7):
+                    regroup(r)
+            if b % 4 == 3 and 7 <= b <= 39:
+                norms((b - 7) // 4)
+            if b % 4 == 0 and 12 <= b <= 36:
+                pair_terms((b - 8) // 4)
+            if j > 0:
                 squared_distance(j)
                 if j < 8:
                     dot_and_cosine(j)
@@ -355,24 +361,53 @@ def tile_adaptiveattention_pa_t_kernel(tc, query, key, Wq, bq, Wk, bk, scoring_w
                     clamp_distance(j)
                     pair_terms(j)
                     dot_and_cosine(j)
+                row_maxima(j)
+
+        def shifted_scores(r):
+            nc.scalar.activation(out=sq_all[:, r, :], in_=sq_all[:, r, :], func=ACT.Sqrt, scale=w2sq)
+            if r >= 4:
+                nc.vector.tensor_tensor(out=t_all[:, r, :], in0=t_all[:, r, :], in1=sq_all[:, r, :], op=ALU.subtract)
+            else:
+                for rt in range(4):
+                    c = 4 * r + rt
+                    part = slice(LK * rt, LK * (rt + 1))
+                    nc.vector.scalar_tensor_tensor(
+                        out=t_all[:, r, part], in0=t_all[:, r, part], scalar=negmax[:, c : c + 1],
+                        in1=sq_all[:, r, part], op0=ALU.add, op1=ALU.subtract,
+                    )
+
+        def softmax_rows(r):
+            if r >= 4:
+                for rt in range(4):
+                    c = 4 * r + rt
+                    nc.scalar.activation(
+                        out=sq_all[:, r, LK * rt : LK * (rt + 1)], in_=t_all[:, r, LK * rt : LK * (rt + 1)],
+                        func=ACT.Exp, bias=negmax[:, c : c + 1], scale=1.0, accum_out=esum[:, c : c + 1],
+                    )
+            else:
+                nc.scalar.activation(out=sq_all[:, r, :], in_=t_all[:, r, :], func=ACT.Exp)
+
+        def row_sums(r):
+            e3 = sq_all[:, r, :].rearrange("p (t j) -> p t j", t=4)
+            if r < 4:
+                nc.vector.tensor_reduce(out=esum[:, 4 * r : 4 * r + 4], in_=e3, axis=AX.X, op=ALU.add)
+
+        def reciprocal_sums(r):
+            nc.vector.reciprocal(out=rsum[:, 4 * r : 4 * r + 4], in_=esum[:, 4 * r : 4 * r + 4])
+
+        def normalise(r):
+            e3 = sq_all[:, r, :].rearrange("p (t j) -> p t j", t=4)
+            for rt in range(4):
+                nc.vector.tensor_scalar(out=e3[:, rt, :], in0=e3[:, rt, :], scalar1=rsum[:, 4 * r + rt : 4 * r + rt + 1], scalar2=None, op0=ALU.mult)
+            nc.sync.dma_start(out=out_blocks[r], in_=e3)
 
         for r in range(8):
-            nc.scalar.activation(out=sq_all[:, r, :], in_=sq_all[:, r, :], func=ACT.Sqrt, scale=w2sq)
-            nc.vector.tensor_tensor(out=t_all[:, r, :], in0=t_all[:, r, :], in1=sq_all[:, r, :], op=ALU.subtract)
-            nc.vector.tensor_reduce(
-                out=negmax[:, 4 * r : 4 * r + 4], in_=t_all[:, r, :].rearrange("p (t j) -> p t j", t=4),
-                axis=AX.X, op=ALU.max, negate=True,
-            )
-        for r in range(8):
-            for rt in range(4):
-                c = 4 * r + rt
-                nc.scalar.activation(
-                    out=sq_all[:, r, LK * rt : LK * (rt + 1)], in_=t_all[:, r, LK * rt : LK * (rt + 1)],
-                    func=ACT.Exp, bias=negmax[:, c : c + 1], scale=1.0, accum_out=esum[:, c : c + 1],
-                )
-            nc.vector.reciprocal(out=rsum[:, 4 * r : 4 * r + 4], in_=esum[:, 4 * r : 4 * r + 4])
-            e3 = sq_all[:, r, :].rearrange("p (t j) -> p t j", t=4)
-            nc.vector.tensor_tensor(
-                out=e3, in0=e3, in1=rsum[:, 4 * r : 4 * r + 4].unsqueeze(2).to_broadcast([P, 4, LK]), op=ALU.mult
-            )
-            nc.sync.dma_start(out=out_blocks[r], in_=e3)
+            shifted_scores(r)
+        for r in range(9):
+            if r < 8:
+                softmax_rows(r)
+                row_sums(r)
+            if r > 0:
+                normalise(r - 1)
+            if r < 8:
+                reciprocal_sums(r)

@@ -21,9 +21,10 @@ G = 2
 FT = 8
 RB = 512
 NBLK = 9
+SLOTS = 8 * NBLK
 S_RING = 5
 V_RING = 3
-W_LEAD = 5
+W_LEAD = 6
 Q_LEAD = 3
 EPS = 1e-8
 
@@ -47,20 +48,21 @@ def tile_adaptiveattention_pa_t_kernel(tc, query, key, Wq, bq, Wk, bk, scoring_w
         wk_view = Wk.rearrange("(t p) k -> p t k", p=P)
         wq_view = Wq.rearrange("(t p) k -> p t k", p=P)
 
-        wk_nat = wpool.tile([P, FT, D], BF16, name="wk_nat")
-        wq_nat = wpool.tile([P, FT, D], BF16, name="wq_nat")
+        wk_nat = wpool.tile([P, FT, D], BF16, name="wk_nat", tag="wnat", bufs=2)
+        wq_nat = wpool.tile([P, FT, D], BF16, name="wq_nat", tag="wnat", bufs=2)
         x_nat = {}
 
         def load_block(i):
             t = xpool.tile([P, 4, D], BF16, name="x_nat%d" % i, tag="x_nat", bufs=3)
             view = key_view if i == 0 else q_blocks[i - 1]
-            for c in range(0, 4, 2):
-                nc.sync.dma_start(out=t[:, c : c + 2, :], in_=view[:, c : c + 2, :])
+            w = 1 if i == 0 else 2
+            for c in range(0, 4, w):
+                nc.sync.dma_start(out=t[:, c : c + w, :], in_=view[:, c : c + w, :])
             x_nat[i] = t
 
         def load_weights(nat, view):
-            for c in range(0, FT, 2):
-                nc.sync.dma_start(out=nat[:, c : c + 2, :], in_=view[:, c : c + 2, :])
+            for c in range(FT):
+                nc.sync.dma_start(out=nat[:, c, :], in_=view[:, c, :])
 
         brow = const.tile([P, P], BF16, name="brow")
         nc.vector.memset(brow[:], 0.0)
@@ -273,14 +275,12 @@ def tile_adaptiveattention_pa_t_kernel(tc, query, key, Wq, bq, Wk, bk, scoring_w
                     out=part, in0=part, scalar1=n2[:, c : c + 1], scalar2=0.0, op0=ALU.add, op1=ALU.max
                 )
 
-        def row_maxima(i):
-            r = i - 1
+        def row_maxima(j):
             nc.vector.tensor_reduce(
-                out=negmax[:, 4 * r : 4 * r + 4], in_=t_all[:, r, :].rearrange("p (t j) -> p t j", t=4),
+                out=negmax[:, 4 * j - 4 : 4 * j], in_=t_all[:, j - 1, :].rearrange("p (t j) -> p t j", t=4),
                 axis=AX.X, op=ALU.max, negate=True,
             )
 
-        n_step = 2 * NBLK
         bias_f = const.tile([P, P], F32, name="bias_f")
         nc.vector.tensor_copy(out=bias_f[:], in_=brow[:])
         bias_ps = psum.tile([P, 4, P], F32, name="bias_ps", tag="v_ring", bufs=V_RING)
@@ -288,41 +288,50 @@ def tile_adaptiveattention_pa_t_kernel(tc, query, key, Wq, bq, Wk, bk, scoring_w
         bias_col = const.tile([P, 16], F32, name="bias_col")
         nc.vector.tensor_copy(out=bias_col[:], in_=bias_ps[:, 0, 0:16])
 
+        on_scalar_weights = (0, 1, 2, 4)
+        on_scalar_inputs = (0, 2, 5, 7)
         for tau in range(4):
-            input_tile(tau, tau % 2 == 0)
+            input_tile(tau, tau in on_scalar_inputs)
         for m in range(W_LEAD):
-            weight_tile(m, m % 2 == 0 and m < 4)
+            weight_tile(m, m in on_scalar_weights)
             if m == 0:
                 quantise_x(0)
-        for m in range(Q_LEAD):
-            quantise_weight_tile(m)
-        tau = 4
-        for b in range(2 * n_step + 9):
-            s, hb = b // 2, b % 2
-            j = (b - 11) // 4 if b >= 15 and b % 4 == 3 else 0
-            if s < n_step:
-                for u in (2 * hb, 2 * hb + 1):
-                    project(s // 2, 4 * (s % 2) + u)
-            if j > 0:
-                dot(j)
-            if b in (3, 7):
-                quantise_x((b + 1) // 4)
-            elif b % 4 == 1 and 9 <= b <= 29:
-                quantise_x((b + 3) // 4)
-            for m in (2 * b + Q_LEAD, 2 * b + Q_LEAD + 1):
-                if m < 2 * FT:
-                    quantise_weight_tile(m)
-            for m in (2 * b + W_LEAD, 2 * b + W_LEAD + 1):
-                if m < 2 * FT:
-                    weight_tile(m, False)
-            for u in range(0 if b in (0, 3) else 2 if b in (1, 2, 6, 7, 8) else 1):
-                if tau < 4 * NBLK:
-                    input_tile(tau, tau in (5, 7))
-                    tau += 1
-            if 1 <= s <= n_step:
-                for rt in (2 * hb, 2 * hb + 1):
-                    norm_tile(s - 1, rt)
-            if b == 3:
+            if m >= W_LEAD - Q_LEAD:
+                quantise_weight_tile(m - (W_LEAD - Q_LEAD))
+
+        def input_slot(tau):
+            return tau - 3 if tau < 8 else tau + 2 if tau < 16 else 2 * tau - 12
+
+        def regroup_slot(s):
+            return max(4 * s + 7, 3 * s + 11)
+
+        def quantise_slot(s):
+            return max(4 * s + 9, 3 * s + 14)
+
+        for beat in range(SLOTS // 2 + 8):
+            slots = (2 * beat, 2 * beat + 1)
+            dot_block = (slots[0] - 22) // 8 if slots[0] >= 30 and slots[0] % 8 == 6 else 0
+            for n in slots:
+                if n < SLOTS:
+                    project(n // 8, n % 8)
+            if dot_block:
+                dot(dot_block)
+            for i in range(1, NBLK):
+                if input_slot(4 * i + 3) + 2 in slots:
+                    quantise_x(i)
+            for n in slots:
+                if n + Q_LEAD < 2 * FT:
+                    quantise_weight_tile(n + Q_LEAD)
+            for n in slots:
+                if n + W_LEAD < 2 * FT:
+                    weight_tile(n + W_LEAD, n + W_LEAD in on_scalar_weights)
+            for tau in range(4, 4 * NBLK):
+                if input_slot(tau) in slots:
+                    input_tile(tau, tau in on_scalar_inputs)
+            for n in slots:
+                if 4 <= n < SLOTS + 4:
+                    norm_tile(n // 4 - 1, n % 4)
+            if beat == 3:
                 wc = const.tile([P, 8], F32, name="wc")
                 sw_f = const.tile([P, 3], F32, name="sw_f")
                 sw_m = const.tile([P, 1], F32, name="sw_m")
@@ -340,32 +349,31 @@ def tile_adaptiveattention_pa_t_kernel(tc, query, key, Wq, bq, Wk, bk, scoring_w
                 w1c = wc[:, 1:2]
                 w2sq = wc[:, 3:4]
                 w1cap = wc[:, 4:5]
-            if b == 12:
+            if beat == 11:
                 spread_key_norms()
-            for r in range(n_step):
-                if b == max(2 * r + 5, r + 9):
-                    quantise_q(r)
-            for r in range(n_step):
-                if b == max(2 * r + 3, r + 7):
-                    regroup(r)
-            if b % 4 == 3 and 7 <= b <= 39:
-                norms((b - 7) // 4)
-            if b % 4 == 0 and 12 <= b <= 36:
-                pair_terms((b - 8) // 4)
-            if j > 0:
-                squared_distance(j)
-                if j < 8:
-                    dot_and_cosine(j)
-                    clamp_distance(j)
-                else:
-                    clamp_distance(j)
-                    pair_terms(j)
-                    dot_and_cosine(j)
-                row_maxima(j)
+            for s in range(2 * NBLK):
+                if quantise_slot(s) in slots:
+                    quantise_q(s)
+            for s in range(2 * NBLK):
+                if regroup_slot(s) in slots:
+                    regroup(s)
+            for i in range(NBLK):
+                if 8 * i + 13 in slots:
+                    norms(i)
+            for i in range(1, NBLK - 1):
+                if 8 * i + 15 in slots:
+                    pair_terms(i)
+            if dot_block:
+                squared_distance(dot_block)
+                if dot_block < NBLK - 1:
+                    dot_and_cosine(dot_block)
+                clamp_distance(dot_block)
+                if dot_block < NBLK - 1:
+                    row_maxima(dot_block)
 
         def shifted_scores(r):
             nc.scalar.activation(out=sq_all[:, r, :], in_=sq_all[:, r, :], func=ACT.Sqrt, scale=w2sq)
-            if r >= 4:
+            if r % 2 == 1 or r == 6:
                 nc.vector.tensor_tensor(out=t_all[:, r, :], in0=t_all[:, r, :], in1=sq_all[:, r, :], op=ALU.subtract)
             else:
                 for rt in range(4):
@@ -377,7 +385,7 @@ def tile_adaptiveattention_pa_t_kernel(tc, query, key, Wq, bq, Wk, bk, scoring_w
                     )
 
         def softmax_rows(r):
-            if r >= 4:
+            if r % 2 == 1 or r == 6:
                 for rt in range(4):
                     c = 4 * r + rt
                     nc.scalar.activation(
@@ -389,7 +397,7 @@ def tile_adaptiveattention_pa_t_kernel(tc, query, key, Wq, bq, Wk, bk, scoring_w
 
         def row_sums(r):
             e3 = sq_all[:, r, :].rearrange("p (t j) -> p t j", t=4)
-            if r < 4:
+            if not (r % 2 == 1 or r == 6):
                 nc.vector.tensor_reduce(out=esum[:, 4 * r : 4 * r + 4], in_=e3, axis=AX.X, op=ALU.add)
 
         def reciprocal_sums(r):
@@ -403,6 +411,10 @@ def tile_adaptiveattention_pa_t_kernel(tc, query, key, Wq, bq, Wk, bk, scoring_w
 
         for r in range(8):
             shifted_scores(r)
+            if r == 3:
+                pair_terms(8)
+                dot_and_cosine(8)
+                row_maxima(8)
         for r in range(9):
             if r < 8:
                 softmax_rows(r)

@@ -24,7 +24,7 @@ NBLK = 9
 SLOTS = 8 * NBLK
 S_RING = 5
 V_RING = 3
-W_LEAD = 6
+W_LEAD = 5
 Q_LEAD = 3
 EPS = 1e-8
 
@@ -55,14 +55,13 @@ def tile_adaptiveattention_pa_t_kernel(tc, query, key, Wq, bq, Wk, bk, scoring_w
         def load_block(i):
             t = xpool.tile([P, 4, D], BF16, name="x_nat%d" % i, tag="x_nat", bufs=3)
             view = key_view if i == 0 else q_blocks[i - 1]
-            w = 1 if i == 0 else 2
-            for c in range(0, 4, w):
-                nc.sync.dma_start(out=t[:, c : c + w, :], in_=view[:, c : c + w, :])
+            for c in range(0, 4, 2):
+                nc.sync.dma_start(out=t[:, c : c + 2, :], in_=view[:, c : c + 2, :])
             x_nat[i] = t
 
         def load_weights(nat, view):
-            for c in range(FT):
-                nc.sync.dma_start(out=nat[:, c, :], in_=view[:, c, :])
+            for c in range(0, FT, 2):
+                nc.sync.dma_start(out=nat[:, c : c + 2, :], in_=view[:, c : c + 2, :])
 
         brow = const.tile([P, P], BF16, name="brow")
         nc.vector.memset(brow[:], 0.0)
@@ -289,15 +288,7 @@ def tile_adaptiveattention_pa_t_kernel(tc, query, key, Wq, bq, Wk, bk, scoring_w
         nc.vector.tensor_copy(out=bias_col[:], in_=bias_ps[:, 0, 0:16])
 
         on_scalar_weights = (0, 1, 2, 4)
-        on_scalar_inputs = (0, 2, 5, 7)
-        for tau in range(4):
-            input_tile(tau, tau in on_scalar_inputs)
-        for m in range(W_LEAD):
-            weight_tile(m, m in on_scalar_weights)
-            if m == 0:
-                quantise_x(0)
-            if m >= W_LEAD - Q_LEAD:
-                quantise_weight_tile(m - (W_LEAD - Q_LEAD))
+        on_scalar_inputs = (1, 3, 5, 7)
 
         def input_slot(tau):
             return tau - 3 if tau < 8 else tau + 2 if tau < 16 else 2 * tau - 12
@@ -308,16 +299,25 @@ def tile_adaptiveattention_pa_t_kernel(tc, query, key, Wq, bq, Wk, bk, scoring_w
         def quantise_slot(s):
             return max(4 * s + 9, 3 * s + 14)
 
-        for beat in range(SLOTS // 2 + 8):
-            slots = (2 * beat, 2 * beat + 1)
-            dot_block = (slots[0] - 22) // 8 if slots[0] >= 30 and slots[0] % 8 == 6 else 0
+        for tau in range(4):
+            input_tile(tau, tau in on_scalar_inputs)
+        for m in range(W_LEAD):
+            weight_tile(m, m in on_scalar_weights)
+            if m == 0:
+                quantise_x(0)
+            if 0 <= m - 2 < Q_LEAD:
+                quantise_weight_tile(m - 2)
+
+        groups = [range(n, n + 2) for n in range(0, 24, 2)] + [range(n, n + 4) for n in range(24, SLOTS + 16, 4)]
+        for slots in groups:
+            due = [i for i in range(1, NBLK) if 8 * i + 22 in slots]
             for n in slots:
                 if n < SLOTS:
                     project(n // 8, n % 8)
-            if dot_block:
-                dot(dot_block)
+            for i in due:
+                dot(i)
             for i in range(1, NBLK):
-                if input_slot(4 * i + 3) + 2 in slots:
+                if input_slot(4 * i + 3) + (2 if i < 3 else 4) in slots:
                     quantise_x(i)
             for n in slots:
                 if n + Q_LEAD < 2 * FT:
@@ -325,13 +325,13 @@ def tile_adaptiveattention_pa_t_kernel(tc, query, key, Wq, bq, Wk, bk, scoring_w
             for n in slots:
                 if n + W_LEAD < 2 * FT:
                     weight_tile(n + W_LEAD, n + W_LEAD in on_scalar_weights)
-            for tau in range(4, 4 * NBLK):
+            for tau in range(4, 8):
                 if input_slot(tau) in slots:
                     input_tile(tau, tau in on_scalar_inputs)
             for n in slots:
                 if 4 <= n < SLOTS + 4:
                     norm_tile(n // 4 - 1, n % 4)
-            if beat == 3:
+            if 7 in slots:
                 wc = const.tile([P, 8], F32, name="wc")
                 sw_f = const.tile([P, 3], F32, name="sw_f")
                 sw_m = const.tile([P, 1], F32, name="sw_m")
@@ -349,7 +349,7 @@ def tile_adaptiveattention_pa_t_kernel(tc, query, key, Wq, bq, Wk, bk, scoring_w
                 w1c = wc[:, 1:2]
                 w2sq = wc[:, 3:4]
                 w1cap = wc[:, 4:5]
-            if beat == 11:
+            if 20 in slots:
                 spread_key_norms()
             for s in range(2 * NBLK):
                 if quantise_slot(s) in slots:
@@ -358,18 +358,21 @@ def tile_adaptiveattention_pa_t_kernel(tc, query, key, Wq, bq, Wk, bk, scoring_w
                 if regroup_slot(s) in slots:
                     regroup(s)
             for i in range(NBLK):
-                if 8 * i + 13 in slots:
+                if 8 * i + 16 in slots:
                     norms(i)
             for i in range(1, NBLK - 1):
-                if 8 * i + 15 in slots:
+                if 8 * i + 18 in slots:
                     pair_terms(i)
-            if dot_block:
-                squared_distance(dot_block)
-                if dot_block < NBLK - 1:
-                    dot_and_cosine(dot_block)
-                clamp_distance(dot_block)
-                if dot_block < NBLK - 1:
-                    row_maxima(dot_block)
+            for i in due:
+                squared_distance(i)
+                if i < NBLK - 1:
+                    dot_and_cosine(i)
+                clamp_distance(i)
+                if i < NBLK - 1:
+                    row_maxima(i)
+            for tau in range(8, 4 * NBLK):
+                if input_slot(tau) in slots:
+                    input_tile(tau, tau in on_scalar_inputs)
 
         def shifted_scores(r):
             nc.scalar.activation(out=sq_all[:, r, :], in_=sq_all[:, r, :], func=ACT.Sqrt, scale=w2sq)

@@ -106,8 +106,8 @@ def tile_adaptiveattention_pa_t_kernel(tc, query, key, Wq, bq, Wk, bk, scoring_w
         w_scales = {}
         w_nat = {"k": wk_nat, "q": wq_nat}
         for label in ("k", "q"):
-            w_codes[label] = wpool.tile([P, G, D], U32, name="w_codes" + label, align_bytes=64)
-            w_scales[label] = wpool.tile([P, G, D], U8, name="w_scales" + label, align_bytes=64)
+            w_codes[label] = wpool.tile([P, G, D], U32, name="w_codes" + label, align_bytes=256)
+            w_scales[label] = wpool.tile([P, G, D], U8, name="w_scales" + label, align_bytes=256)
 
         def weight_tile(m, on_scalar):
             label, t = "kq"[m // FT], m % FT
@@ -131,8 +131,8 @@ def tile_adaptiveattention_pa_t_kernel(tc, query, key, Wq, bq, Wk, bk, scoring_w
             i, rt = tau // 4, tau % 4
             if rt == 0:
                 x_grp[i] = xpool.tile([P, G * RB * 4], BF16, name="x_grp%d" % i, tag="x_grp", bufs=3, align_bytes=64)
-                x_codes[i] = xpool.tile([P, G, RB], U32, name="x_codes%d" % i, tag="x_codes", bufs=3, align_bytes=64)
-                x_scales[i] = xpool.tile([P, G, RB], U8, name="x_scales%d" % i, tag="x_scales", bufs=3, align_bytes=64)
+                x_codes[i] = xpool.tile([P, G, RB], U32, name="x_codes%d" % i, tag="x_codes", bufs=3, align_bytes=256)
+                x_scales[i] = xpool.tile([P, G, RB], U8, name="x_scales%d" % i, tag="x_scales", bufs=3, align_bytes=256)
             transpose_tile(x_nat[i][:, rt, :], words(x_grp[i])[:, :, P * rt : P * (rt + 1), :], on_scalar)
             if rt == 3 and i + 3 < NBLK:
                 load_block(i + 3)
@@ -151,8 +151,8 @@ def tile_adaptiveattention_pa_t_kernel(tc, query, key, Wq, bq, Wk, bk, scoring_w
         negmax = fin.tile([P, 32], F32, name="negmax")
         esum = fin.tile([P, 32], F32, name="esum")
         rsum = fin.tile([P, 32], F32, name="rsum")
-        k_codes = fin.tile([P, G, RB], U32, name="k_codes", align_bytes=64)
-        k_scales = fin.tile([P, G, RB], U8, name="k_scales", align_bytes=64)
+        k_codes = fin.tile([P, G, RB], U32, name="k_codes", align_bytes=256)
+        k_scales = fin.tile([P, G, RB], U8, name="k_scales", align_bytes=256)
 
         qf = {}
         q_grp = {}
@@ -206,8 +206,8 @@ def tile_adaptiveattention_pa_t_kernel(tc, query, key, Wq, bq, Wk, bk, scoring_w
         def quantise_q(s):
             i, h = s // 2, s % 2
             if i > 0 and h == 0:
-                q_codes[i] = qpool.tile([P, G, RB], U32, name="q_codes%d" % i, tag="q_codes", align_bytes=64)
-                q_scales[i] = qpool.tile([P, G, RB], U8, name="q_scales%d" % i, tag="q_scales", align_bytes=64)
+                q_codes[i] = qpool.tile([P, G, RB], U32, name="q_codes%d" % i, tag="q_codes", align_bytes=256)
+                q_scales[i] = qpool.tile([P, G, RB], U8, name="q_scales%d" % i, tag="q_scales", align_bytes=256)
             nc.vector.quantize_mx(
                 out=q_codes[i][:, h, :].bitcast(FP8X4), scales=q_scales[i][:, h, :], in_=q_grp[s][:]
             )
@@ -287,17 +287,35 @@ def tile_adaptiveattention_pa_t_kernel(tc, query, key, Wq, bq, Wk, bk, scoring_w
         bias_col = const.tile([P, 16], F32, name="bias_col")
         nc.vector.tensor_copy(out=bias_col[:], in_=bias_ps[:, 0, 0:16])
 
-        on_scalar_weights = (0, 1, 2, 4)
+        wc = const.tile([P, 8], F32, name="wc")
+        sw_f = const.tile([P, 3], F32, name="sw_f")
+        sw_m = const.tile([P, 1], F32, name="sw_m")
+        sw_s = const.tile([P, 1], F32, name="sw_s")
+        sw_r = const.tile([P, 1], F32, name="sw_r")
+        sw_e = const.tile([P, 3], F32, name="sw_e")
+        nc.vector.tensor_copy(out=sw_f[:], in_=sw_b[:])
+        nc.vector.tensor_reduce(out=sw_m[:], in_=sw_f[:], axis=AX.X, op=ALU.max, negate=True)
+        nc.scalar.activation(out=sw_e[:], in_=sw_f[:], func=ACT.Exp, bias=sw_m[:], scale=1.0, accum_out=sw_s[:])
+        nc.vector.reciprocal(out=sw_r[:], in_=sw_s[:])
+        nc.vector.tensor_scalar(out=wc[:, 0:3], in0=sw_e[:], scalar1=sw_r[:], scalar2=None, op0=ALU.mult)
+        nc.vector.tensor_tensor(out=wc[:, 3:4], in0=wc[:, 2:3], in1=wc[:, 2:3], op=ALU.mult)
+        nc.vector.tensor_scalar(out=wc[:, 4:5], in0=wc[:, 1:2], scalar1=1.0 / EPS, scalar2=None, op0=ALU.mult)
+        w0c = wc[:, 0:1]
+        w1c = wc[:, 1:2]
+        w2sq = wc[:, 3:4]
+        w1cap = wc[:, 4:5]
+
+        on_scalar_weights = (0, 1, 2, 3)
         on_scalar_inputs = (1, 3, 5, 7)
 
         def input_slot(tau):
-            return tau - 3 if tau < 8 else tau + 2 if tau < 16 else 2 * tau - 12
+            return tau - 3 if tau < 8 else tau + 1 if tau < 12 else tau + 2 if tau < 16 else 2 * tau - 12
 
         def regroup_slot(s):
-            return max(4 * s + 7, 3 * s + 11)
+            return max(4 * s + 6, 3 * s + 11)
 
         def quantise_slot(s):
-            return max(4 * s + 9, 3 * s + 14)
+            return max(4 * s + 8, 3 * s + 14)
 
         for tau in range(4):
             input_tile(tau, tau in on_scalar_inputs)
@@ -331,24 +349,6 @@ def tile_adaptiveattention_pa_t_kernel(tc, query, key, Wq, bq, Wk, bk, scoring_w
             for n in slots:
                 if 4 <= n < SLOTS + 4:
                     norm_tile(n // 4 - 1, n % 4)
-            if 7 in slots:
-                wc = const.tile([P, 8], F32, name="wc")
-                sw_f = const.tile([P, 3], F32, name="sw_f")
-                sw_m = const.tile([P, 1], F32, name="sw_m")
-                sw_s = const.tile([P, 1], F32, name="sw_s")
-                sw_r = const.tile([P, 1], F32, name="sw_r")
-                sw_e = const.tile([P, 3], F32, name="sw_e")
-                nc.vector.tensor_copy(out=sw_f[:], in_=sw_b[:])
-                nc.vector.tensor_reduce(out=sw_m[:], in_=sw_f[:], axis=AX.X, op=ALU.max, negate=True)
-                nc.scalar.activation(out=sw_e[:], in_=sw_f[:], func=ACT.Exp, bias=sw_m[:], scale=1.0, accum_out=sw_s[:])
-                nc.vector.reciprocal(out=sw_r[:], in_=sw_s[:])
-                nc.vector.tensor_scalar(out=wc[:, 0:3], in0=sw_e[:], scalar1=sw_r[:], scalar2=None, op0=ALU.mult)
-                nc.vector.tensor_tensor(out=wc[:, 3:4], in0=wc[:, 2:3], in1=wc[:, 2:3], op=ALU.mult)
-                nc.vector.tensor_scalar(out=wc[:, 4:5], in0=wc[:, 1:2], scalar1=1.0 / EPS, scalar2=None, op0=ALU.mult)
-                w0c = wc[:, 0:1]
-                w1c = wc[:, 1:2]
-                w2sq = wc[:, 3:4]
-                w1cap = wc[:, 4:5]
             if 20 in slots:
                 spread_key_norms()
             for s in range(2 * NBLK):
@@ -361,7 +361,7 @@ def tile_adaptiveattention_pa_t_kernel(tc, query, key, Wq, bq, Wk, bk, scoring_w
                 if 8 * i + 16 in slots:
                     norms(i)
             for i in range(1, NBLK - 1):
-                if 8 * i + 18 in slots:
+                if 8 * i + 19 in slots:
                     pair_terms(i)
             for i in due:
                 squared_distance(i)
@@ -376,7 +376,7 @@ def tile_adaptiveattention_pa_t_kernel(tc, query, key, Wq, bq, Wk, bk, scoring_w
 
         def shifted_scores(r):
             nc.scalar.activation(out=sq_all[:, r, :], in_=sq_all[:, r, :], func=ACT.Sqrt, scale=w2sq)
-            if r % 2 == 1 or r == 6:
+            if r % 2 == 0 or r == 7:
                 nc.vector.tensor_tensor(out=t_all[:, r, :], in0=t_all[:, r, :], in1=sq_all[:, r, :], op=ALU.subtract)
             else:
                 for rt in range(4):
@@ -388,7 +388,7 @@ def tile_adaptiveattention_pa_t_kernel(tc, query, key, Wq, bq, Wk, bk, scoring_w
                     )
 
         def softmax_rows(r):
-            if r % 2 == 1 or r == 6:
+            if r % 2 == 0 or r == 7:
                 for rt in range(4):
                     c = 4 * r + rt
                     nc.scalar.activation(
@@ -399,30 +399,37 @@ def tile_adaptiveattention_pa_t_kernel(tc, query, key, Wq, bq, Wk, bk, scoring_w
                 nc.scalar.activation(out=sq_all[:, r, :], in_=t_all[:, r, :], func=ACT.Exp)
 
         def row_sums(r):
-            e3 = sq_all[:, r, :].rearrange("p (t j) -> p t j", t=4)
-            if not (r % 2 == 1 or r == 6):
+            if not (r % 2 == 0 or r == 7):
+                e3 = sq_all[:, r, :].rearrange("p (t j) -> p t j", t=4)
                 nc.vector.tensor_reduce(out=esum[:, 4 * r : 4 * r + 4], in_=e3, axis=AX.X, op=ALU.add)
 
-        def reciprocal_sums(r):
-            nc.vector.reciprocal(out=rsum[:, 4 * r : 4 * r + 4], in_=esum[:, 4 * r : 4 * r + 4])
+        def reciprocal_sums(r, tiles):
+            c = slice(4 * r + tiles.start, 4 * r + tiles.stop)
+            nc.vector.reciprocal(out=rsum[:, c], in_=esum[:, c])
 
-        def normalise(r):
+        def normalise(r, tiles):
             e3 = sq_all[:, r, :].rearrange("p (t j) -> p t j", t=4)
-            for rt in range(4):
-                nc.vector.tensor_scalar(out=e3[:, rt, :], in0=e3[:, rt, :], scalar1=rsum[:, 4 * r + rt : 4 * r + rt + 1], scalar2=None, op0=ALU.mult)
-            nc.sync.dma_start(out=out_blocks[r], in_=e3)
+            for rt in range(tiles.start, tiles.stop):
+                nc.vector.tensor_scalar(
+                    out=e3[:, rt, :], in0=e3[:, rt, :], scalar1=rsum[:, 4 * r + rt : 4 * r + rt + 1], scalar2=None,
+                    op0=ALU.mult,
+                )
+            nc.sync.dma_start(out=out_blocks[r][:, tiles.start : tiles.stop, :], in_=e3[:, tiles.start : tiles.stop, :])
 
+        whole = range(0, 4)
         for r in range(8):
             shifted_scores(r)
             if r == 3:
                 pair_terms(8)
                 dot_and_cosine(8)
                 row_maxima(8)
-        for r in range(9):
-            if r < 8:
-                softmax_rows(r)
-                row_sums(r)
+        for r in range(8):
+            softmax_rows(r)
+            row_sums(r)
             if r > 0:
-                normalise(r - 1)
-            if r < 8:
-                reciprocal_sums(r)
+                normalise(r - 1, whole)
+            if r < 7:
+                reciprocal_sums(r, whole)
+        for tiles in (range(0, 2), range(2, 4)):
+            reciprocal_sums(7, tiles)
+            normalise(7, tiles)

@@ -280,6 +280,12 @@ def tile_adaptiveattention_pa_t_kernel(tc, query, key, Wq, bq, Wk, bk, scoring_w
                 axis=AX.X, op=ALU.max, negate=True,
             )
 
+        zeros = const.tile([P, RB], BF16, name="zeros")
+        nc.vector.memset(zeros[:], 0.0)
+        warm = psum.tile([P, RB], F32, name="warm", tag="v_ring", bufs=V_RING)
+        for u in range(5):
+            nc.tensor.matmul(out=warm[:], lhsT=zeros[:, 0:P], rhs=zeros[:], start=True, stop=True)
+
         bias_f = const.tile([P, P], F32, name="bias_f")
         nc.vector.tensor_copy(out=bias_f[:], in_=brow[:])
         bias_ps = psum.tile([P, 4, P], F32, name="bias_ps", tag="v_ring", bufs=V_RING)

@@ -42,11 +42,11 @@ def tile_adaptiveattention_pa_t_kernel(tc, query, key, Wq, bq, Wk, bk, scoring_w
         fin = ctx.enter_context(tc.tile_pool(name="fin", bufs=1))
         psum = ctx.enter_context(tc.psum_pool(name="psum", bufs=1))
 
-        q_blocks = query.rearrange("b (h t p) k -> (b h) p t k", h=2, t=4, p=P)
+        q_blocks = query.rearrange("b (h p t) k -> (b h) p t k", h=2, t=4, p=P)
         key_view = key.rearrange("b p k -> p b k")
-        out_blocks = out.rearrange("b (h t p) j -> (b h) p t j", h=2, t=4, p=P)
-        wk_view = Wk.rearrange("(t p) k -> p t k", p=P)
-        wq_view = Wq.rearrange("(t p) k -> p t k", p=P)
+        out_blocks = out.rearrange("b (h p t) j -> (b h) p t j", h=2, t=4, p=P)
+        wk_view = Wk.rearrange("(p t) k -> p t k", p=P)
+        wq_view = Wq.rearrange("(p t) k -> p t k", p=P)
 
         wk_nat = wpool.tile([P, FT, D], BF16, name="wk_nat", tag="wnat", bufs=2)
         wq_nat = wpool.tile([P, FT, D], BF16, name="wq_nat", tag="wnat", bufs=2)
@@ -63,10 +63,10 @@ def tile_adaptiveattention_pa_t_kernel(tc, query, key, Wq, bq, Wk, bk, scoring_w
             for c in range(0, FT, 2):
                 nc.sync.dma_start(out=nat[:, c : c + 2, :], in_=view[:, c : c + 2, :])
 
-        brow = const.tile([P, P], BF16, name="brow")
-        nc.vector.memset(brow[:], 0.0)
-        nc.sync.dma_start(out=brow[0:8, :], in_=bq.rearrange("(r c) -> r c", c=P))
-        nc.sync.dma_start(out=brow[8:16, :], in_=bk.rearrange("(r c) -> r c", c=P))
+        bias = {}
+        for label, vector in (("k", bk), ("q", bq)):
+            bias[label] = const.tile([P, FT], BF16, name="bias_" + label)
+            nc.sync.dma_start(out=bias[label][:], in_=vector.rearrange("(p t) -> p t", t=FT))
         sw_b = const.tile([P, 3], BF16, name="sw_b")
         nc.sync.dma_start(out=sw_b[:], in_=scoring_weights.partition_broadcast(P))
         load_block(0)
@@ -178,9 +178,8 @@ def tile_adaptiveattention_pa_t_kernel(tc, query, key, Wq, bq, Wk, bk, scoring_w
                     start=(g == 0),
                     stop=(g == G - 1),
                 )
-            col = (8 if i == 0 else 0) + ft
             nc.scalar.activation(
-                out=qf[s][:, ft % 4, :], in_=acc[:], func=ACT.Tanh, bias=bias_col[:, col : col + 1], scale=1.0
+                out=qf[s][:, ft % 4, :], in_=acc[:], func=ACT.Tanh, bias=bias[label][:, ft : ft + 1], scale=1.0
             )
 
         def norm_tile(s, rt):
@@ -286,13 +285,6 @@ def tile_adaptiveattention_pa_t_kernel(tc, query, key, Wq, bq, Wk, bk, scoring_w
         for u in range(5):
             nc.tensor.matmul(out=warm[:], lhsT=zeros[:, 0:P], rhs=zeros[:], start=True, stop=True)
 
-        bias_f = const.tile([P, P], F32, name="bias_f")
-        nc.vector.tensor_copy(out=bias_f[:], in_=brow[:])
-        bias_ps = psum.tile([P, 4, P], F32, name="bias_ps", tag="v_ring", bufs=V_RING)
-        nc.tensor.transpose(bias_ps[:, 0, :], bias_f[:], ident[:])
-        bias_col = const.tile([P, 16], F32, name="bias_col")
-        nc.vector.tensor_copy(out=bias_col[:], in_=bias_ps[:, 0, 0:16])
-
         wc = const.tile([P, 8], F32, name="wc")
         sw_f = const.tile([P, 3], F32, name="sw_f")
         sw_m = const.tile([P, 1], F32, name="sw_m")
@@ -311,17 +303,17 @@ def tile_adaptiveattention_pa_t_kernel(tc, query, key, Wq, bq, Wk, bk, scoring_w
         w2sq = wc[:, 3:4]
         w1cap = wc[:, 4:5]
 
-        on_scalar_weights = (0, 1, 2, 3)
-        on_scalar_inputs = (1, 3, 5, 7)
+        on_scalar_weights = (0, 1, 2)
+        on_scalar_inputs = (1, 3, 5, 7, 9)
 
         def input_slot(tau):
-            return tau - 3 if tau < 8 else tau + 1 if tau < 12 else tau + 2 if tau < 16 else 2 * tau - 12
+            return tau - 4 if tau < 8 else tau + 1 if tau < 16 else 2 * tau - 12
 
         def regroup_slot(s):
             return max(4 * s + 6, 3 * s + 11)
 
         def quantise_slot(s):
-            return max(4 * s + 8, 3 * s + 14)
+            return max(4 * s + 8, 3 * s + 13)
 
         for tau in range(4):
             input_tile(tau, tau in on_scalar_inputs)
@@ -334,7 +326,7 @@ def tile_adaptiveattention_pa_t_kernel(tc, query, key, Wq, bq, Wk, bk, scoring_w
 
         groups = [range(n, n + 2) for n in range(0, 24, 2)] + [range(n, n + 4) for n in range(24, SLOTS + 16, 4)]
         for slots in groups:
-            due = [i for i in range(1, NBLK) if 8 * i + 22 in slots]
+            due = [i for i in range(1, NBLK) if 8 * i + 20 in slots]
             for n in slots:
                 if n < SLOTS:
                     project(n // 8, n % 8)

from contextlib import ExitStack

import concourse.mybir as mybir
from concourse.masks import make_identity

F32 = mybir.dt.float32
BF16 = mybir.dt.bfloat16
U32 = mybir.dt.uint32
U8 = mybir.dt.uint8
FP8X4 = mybir.dt.float8_e4m3fn_x4
ACT = mybir.ActivationFunctionType
ALU = mybir.AluOpType
AX = mybir.AxisListType

P = 128
D = 1024
B = 4
LQ = 1024
LK = 128
G = 2
FT = 8
RB = 512
NBLK = 9
SLOTS = 8 * NBLK
S_RING = 5
V_RING = 3
W_LEAD = 5
Q_LEAD = 3
EPS = 1e-8

FLOPS = 2 * (B * LQ + B * LK) * D * D + 2 * B * LQ * LK * D


def tile_adaptiveattention_pa_t_kernel(tc, query, key, Wq, bq, Wk, bk, scoring_weights, out):
    nc = tc.nc
    with ExitStack() as ctx:
        ctx.enter_context(tc.manual_schedule())
        const = ctx.enter_context(tc.tile_pool(name="const", bufs=1))
        wpool = ctx.enter_context(tc.tile_pool(name="wpool", bufs=1))
        xpool = ctx.enter_context(tc.tile_pool(name="xpool", bufs=2))
        qpool = ctx.enter_context(tc.tile_pool(name="qpool", bufs=2))
        fin = ctx.enter_context(tc.tile_pool(name="fin", bufs=1))
        psum = ctx.enter_context(tc.psum_pool(name="psum", bufs=1))

        q_blocks = query.rearrange("b (h p t) k -> (b h) p t k", h=2, t=4, p=P)
        key_view = key.rearrange("b p k -> p b k")
        out_blocks = out.rearrange("b (h p t) j -> (b h) p t j", h=2, t=4, p=P)
        wk_view = Wk.rearrange("(p t) k -> p t k", p=P)
        wq_view = Wq.rearrange("(p t) k -> p t k", p=P)

        wk_nat = wpool.tile([P, FT, D], BF16, name="wk_nat", tag="wnat", bufs=2)
        wq_nat = wpool.tile([P, FT, D], BF16, name="wq_nat", tag="wnat", bufs=2)
        x_nat = {}

        def load_block(i):
            t = xpool.tile([P, 4, D], BF16, name="x_nat%d" % i, tag="x_nat", bufs=3)
            view = key_view if i == 0 else q_blocks[i - 1]
            for c in range(0, 4, 2):
                nc.sync.dma_start(out=t[:, c : c + 2, :], in_=view[:, c : c + 2, :])
            x_nat[i] = t

        def load_weights(nat, view):
            for c in range(0, FT, 2):
                nc.sync.dma_start(out=nat[:, c : c + 2, :], in_=view[:, c : c + 2, :])

        bias = {}
        for label, vector in (("k", bk), ("q", bq)):
            bias[label] = const.tile([P, FT], BF16, name="bias_" + label)
            nc.sync.dma_start(out=bias[label][:], in_=vector.rearrange("(p t) -> p t", t=FT))
        sw_b = const.tile([P, 3], BF16, name="sw_b")
        nc.sync.dma_start(out=sw_b[:], in_=scoring_weights.partition_broadcast(P))
        load_block(0)
        load_weights(wk_nat, wk_view)
        load_block(1)
        load_weights(wq_nat, wq_view)
        load_block(2)

        ident = const.tile([P, P], F32, name="ident")
        make_identity(nc, ident[:])
        neghalf = const.tile([P, 4], F32, name="neghalf")
        nc.gpsimd.memset(neghalf[:], -0.5)

        def words(grp):
            return grp[:].bitcast(F32).rearrange("p (g r u) -> p g r u", g=G, u=2)

        def transpose_tile(nat_row_tile, dst, on_scalar):
            ps = psum.tile([P, 4, P], F32, name="tr_ps", tag="s_ring" if on_scalar else "v_ring", bufs=S_RING if on_scalar else V_RING)
            src = nat_row_tile.bitcast(F32)
            for j in range(4):
                nc.tensor.transpose(ps[:, j, :], src[:, P * j : P * (j + 1)], ident[:])
            view = ps[:].rearrange("p (g u) r -> p g r u", g=G)
            if on_scalar:
                nc.scalar.copy(out=dst, in_=view)
            else:
                nc.vector.tensor_copy(out=dst, in_=view)

        def quantise(grp, rows, codes, scales, g, c0, c1):
            nc.vector.quantize_mx(
                out=codes[:, g, c0:c1].bitcast(FP8X4),
                scales=scales[:, g, c0:c1],
                in_=grp[:, (g * rows + c0) * 4 : (g * rows + c1) * 4],
            )

        w_grp = {}
        w_codes = {}
        w_scales = {}
        w_nat = {"k": wk_nat, "q": wq_nat}
        for label in ("k", "q"):
            w_codes[label] = wpool.tile([P, G, D], U32, name="w_codes" + label, align_bytes=256)
            w_scales[label] = wpool.tile([P, G, D], U8, name="w_scales" + label, align_bytes=256)

        def weight_tile(m, on_scalar):
            label, t = "kq"[m // FT], m % FT
            w_grp[m] = wpool.tile([P, G * P * 4], BF16, name="w_grp%d" % m, tag="w_grp", bufs=6, align_bytes=64)
            transpose_tile(w_nat[label][:, t, :], words(w_grp[m]), on_scalar)

        def quantise_weight_tile(m):
            label, t = "kq"[m // FT], m % FT
            for g in range(G):
                nc.vector.quantize_mx(
                    out=w_codes[label][:, g, P * t : P * (t + 1)].bitcast(FP8X4),
                    scales=w_scales[label][:, g, P * t : P * (t + 1)],
                    in_=w_grp[m][:, g * P * 4 : (g + 1) * P * 4],
                )

        x_grp = {}
        x_codes = {}
        x_scales = {}

        def input_tile(tau, on_scalar):
            i, rt = tau // 4, tau % 4
            if rt == 0:
                x_grp[i] = xpool.tile([P, G * RB * 4], BF16, name="x_grp%d" % i, tag="x_grp", bufs=3, align_bytes=64)
                x_codes[i] = xpool.tile([P, G, RB], U32, name="x_codes%d" % i, tag="x_codes", bufs=3, align_bytes=256)
                x_scales[i] = xpool.tile([P, G, RB], U8, name="x_scales%d" % i, tag="x_scales", bufs=3, align_bytes=256)
            transpose_tile(x_nat[i][:, rt, :], words(x_grp[i])[:, :, P * rt : P * (rt + 1), :], on_scalar)
            if rt == 3 and i + 3 < NBLK:
                load_block(i + 3)

        def quantise_x(i):
            for g in range(G):
                quantise(x_grp[i], RB, x_codes[i], x_scales[i], g, 0, RB)

        n2p = fin.tile([P, 4 * NBLK, 2], F32, name="n2p")
        n2 = fin.tile([P, 4 * NBLK], F32, name="n2")
        rn = fin.tile([P, 4 * NBLK], F32, name="rn")
        kn2_bc = fin.tile([P, B, LK], F32, name="kn2_bc")
        rkn_bc = fin.tile([P, B, LK], F32, name="rkn_bc")
        sq_all = fin.tile([P, 8, RB], F32, name="sq_all")
        t_all = fin.tile([P, 8, RB], F32, name="t_all")
        negmax = fin.tile([P, 32], F32, name="negmax")
        esum = fin.tile([P, 32], F32, name="esum")
        rsum = fin.tile([P, 32], F32, name="rsum")
        k_codes = fin.tile([P, G, RB], U32, name="k_codes", align_bytes=256)
        k_scales = fin.tile([P, G, RB], U8, name="k_scales", align_bytes=256)

        qf = {}
        q_grp = {}
        q_codes = {0: k_codes}
        q_scales = {0: k_scales}
        r_cos = {}
        dots = {}

        def project(i, ft):
            s = 2 * i + ft // 4
            if ft % 4 == 0:
                qf[s] = qpool.tile([P, 4, RB], F32, name="qf%d" % s, tag="qf", bufs=5)
            label = "k" if i == 0 else "q"
            wc_, ws_ = w_codes[label], w_scales[label]
            acc = psum.tile([P, RB], F32, name="acc", tag="s_ring", bufs=S_RING)
            for g in range(G):
                nc.tensor.matmul_mx(
                    out=acc[:],
                    lhsT=wc_[:, g, P * ft : P * (ft + 1)].bitcast(FP8X4),
                    lhsT_scale=ws_[:, g, P * ft : P * (ft + 1)],
                    rhs=x_codes[i][:, g, :].bitcast(FP8X4),
                    rhs_scale=x_scales[i][:, g, :],
                    start=(g == 0),
                    stop=(g == G - 1),
                )
            nc.scalar.activation(
                out=qf[s][:, ft % 4, :], in_=acc[:], func=ACT.Tanh, bias=bias[label][:, ft : ft + 1], scale=1.0
            )

        def norm_tile(s, rt):
            i, h = s // 2, s % 2
            pn = psum.tile([P, 4, P], F32, name="pn", tag="s_ring", bufs=S_RING)
            for t in range(4):
                nc.tensor.transpose(pn[:, t, :], qf[s][:, t, P * rt : P * (rt + 1)], ident[:])
            junk = qpool.tile([P, RB], BF16, name="junk", tag="junk")
            nc.scalar.activation(
                out=junk[:],
                in_=pn[:].rearrange("p t f -> p (t f)"),
                func=ACT.Square,
                accum_out=n2p[:, 4 * i + rt, h : h + 1],
            )

        def regroup(s):
            q_grp[s] = qpool.tile([P, RB * 4], BF16, name="q_grp%d" % s, tag="q_grp", align_bytes=64)
            nc.vector.tensor_copy(
                out=q_grp[s][:].rearrange("p (c i t) -> p c t i", i=4, t=4),
                in_=qf[s][:].rearrange("p t (c i) -> p c t i", i=4),
            )

        def quantise_q(s):
            i, h = s // 2, s % 2
            if i > 0 and h == 0:
                q_codes[i] = qpool.tile([P, G, RB], U32, name="q_codes%d" % i, tag="q_codes", align_bytes=256)
                q_scales[i] = qpool.tile([P, G, RB], U8, name="q_scales%d" % i, tag="q_scales", align_bytes=256)
            nc.vector.quantize_mx(
                out=q_codes[i][:, h, :].bitcast(FP8X4), scales=q_scales[i][:, h, :], in_=q_grp[s][:]
            )

        def norms(i):
            c = slice(4 * i, 4 * i + 4)
            nc.gpsimd.tensor_tensor(out=n2[:, c], in0=n2p[:, c, 0], in1=n2p[:, c, 1], op=ALU.add)
            nc.gpsimd.tensor_tensor(out=rn[:, c], in0=n2[:, c], in1=neghalf[:], op=ALU.pow)

        def spread_key_norms():
            for v in range(2):
                ps = psum.tile([P, 4, P], F32, name="kn_ps", tag="v_ring", bufs=V_RING)
                for b in range(B):
                    nc.tensor.transpose(ps[:, b, :], (n2, rn)[v][:, b : b + 1].to_broadcast([P, P]), ident[:])
                if v == 0:
                    nc.vector.tensor_copy(out=kn2_bc[:], in_=ps[:])
                else:
                    nc.vector.tensor_scalar(out=rkn_bc[:], in0=ps[:], scalar1=w1c, scalar2=None, op0=ALU.mult)

        def pair_terms(i):
            b = (i - 1) // 2
            r_cos[i] = qpool.tile([P, 4, LK], F32, name="r_cos%d" % i, tag="r_cos")
            for rt in range(4):
                c = 4 * i + rt
                nc.vector.tensor_scalar(
                    out=r_cos[i][:, rt, :], in0=rkn_bc[:, b, :], scalar1=rn[:, c : c + 1], scalar2=w1cap,
                    op0=ALU.mult, op1=ALU.min,
                )

        def dot(i):
            b = (i - 1) // 2
            pd = psum.tile([P, 4, LK], F32, name="pd", tag="v_ring", bufs=V_RING)
            for rt in range(4):
                for g in range(G):
                    nc.tensor.matmul_mx(
                        out=pd[:, rt, :],
                        lhsT=q_codes[i][:, g, P * rt : P * (rt + 1)].bitcast(FP8X4),
                        lhsT_scale=q_scales[i][:, g, P * rt : P * (rt + 1)],
                        rhs=k_codes[:, g, LK * b : LK * (b + 1)].bitcast(FP8X4),
                        rhs_scale=k_scales[:, g, LK * b : LK * (b + 1)],
                        start=(g == 0),
                        stop=(g == G - 1),
                    )
            dots[i] = pd

        def squared_distance(i):
            b = (i - 1) // 2
            nc.vector.scalar_tensor_tensor(
                out=sq_all[:, i - 1, :].rearrange("p (t j) -> p t j", t=4), in0=dots[i][:], scalar=-2.0,
                in1=kn2_bc[:, b : b + 1, :].to_broadcast([P, 4, LK]), op0=ALU.mult, op1=ALU.add,
            )

        def dot_and_cosine(i):
            nc.vector.scalar_tensor_tensor(
                out=t_all[:, i - 1, :], in0=r_cos[i][:].rearrange("p t j -> p (t j)"), scalar=w0c,
                in1=dots[i][:].rearrange("p t j -> p (t j)"), op0=ALU.add, op1=ALU.mult,
            )

        def clamp_distance(i):
            for rt in range(4):
                c = 4 * i + rt
                part = sq_all[:, i - 1, LK * rt : LK * (rt + 1)]
                nc.vector.tensor_scalar(
                    out=part, in0=part, scalar1=n2[:, c : c + 1], scalar2=0.0, op0=ALU.add, op1=ALU.max
                )

        def row_maxima(j):
            nc.vector.tensor_reduce(
                out=negmax[:, 4 * j - 4 : 4 * j], in_=t_all[:, j - 1, :].rearrange("p (t j) -> p t j", t=4),
                axis=AX.X, op=ALU.max, negate=True,
            )

        zeros = const.tile([P, RB], BF16, name="zeros")
        nc.vector.memset(zeros[:], 0.0)
        warm = psum.tile([P, RB], F32, name="warm", tag="v_ring", bufs=V_RING)
        for u in range(5):
            nc.tensor.matmul(out=warm[:], lhsT=zeros[:, 0:P], rhs=zeros[:], start=True, stop=True)

        wc = const.tile([P, 8], F32, name="wc")
        sw_f = const.tile([P, 3], F32, name="sw_f")
        sw_m = const.tile([P, 1], F32, name="sw_m")
        sw_s = const.tile([P, 1], F32, name="sw_s")
        sw_r = const.tile([P, 1], F32, name="sw_r")
        sw_e = const.tile([P, 3], F32, name="sw_e")
        nc.vector.tensor_copy(out=sw_f[:], in_=sw_b[:])
        nc.vector.tensor_reduce(out=sw_m[:], in_=sw_f[:], axis=AX.X, op=ALU.max, negate=True)
        nc.scalar.activation(out=sw_e[:], in_=sw_f[:], func=ACT.Exp, bias=sw_m[:], scale=1.0, accum_out=sw_s[:])
        nc.vector.reciprocal(out=sw_r[:], in_=sw_s[:])
        nc.vector.tensor_scalar(out=wc[:, 0:3], in0=sw_e[:], scalar1=sw_r[:], scalar2=None, op0=ALU.mult)
        nc.vector.tensor_tensor(out=wc[:, 3:4], in0=wc[:, 2:3], in1=wc[:, 2:3], op=ALU.mult)
        nc.vector.tensor_scalar(out=wc[:, 4:5], in0=wc[:, 1:2], scalar1=1.0 / EPS, scalar2=None, op0=ALU.mult)
        w0c = wc[:, 0:1]
        w1c = wc[:, 1:2]
        w2sq = wc[:, 3:4]
        w1cap = wc[:, 4:5]

        on_scalar_weights = (0, 1, 2)
        on_scalar_inputs = (1, 3, 5, 7, 9)

        def input_slot(tau):
            return tau - 4 if tau < 8 else tau + 1 if tau < 16 else 2 * tau - 12

        def regroup_slot(s):
            return max(4 * s + 6, 3 * s + 11)

        def quantise_slot(s):
            return max(4 * s + 8, 3 * s + 13)

        for tau in range(4):
            input_tile(tau, tau in on_scalar_inputs)
        for m in range(W_LEAD):
            weight_tile(m, m in on_scalar_weights)
            if m == 0:
                quantise_x(0)
            if 0 <= m - 2 < Q_LEAD:
                quantise_weight_tile(m - 2)

        groups = [range(n, n + 2) for n in range(0, 24, 2)] + [range(n, n + 4) for n in range(24, SLOTS + 16, 4)]
        for slots in groups:
            due = [i for i in range(1, NBLK) if 8 * i + 20 in slots]
            for n in slots:
                if n < SLOTS:
                    project(n // 8, n % 8)
            for i in due:
                dot(i)
            for i in range(1, NBLK):
                if input_slot(4 * i + 3) + (2 if i < 3 else 4) in slots:
                    quantise_x(i)
            for n in slots:
                if n + Q_LEAD < 2 * FT:
                    quantise_weight_tile(n + Q_LEAD)
            for n in slots:
                if n + W_LEAD < 2 * FT:
                    weight_tile(n + W_LEAD, n + W_LEAD in on_scalar_weights)
            for tau in range(4, 8):
                if input_slot(tau) in slots:
                    input_tile(tau, tau in on_scalar_inputs)
            for n in slots:
                if 4 <= n < SLOTS + 4:
                    norm_tile(n // 4 - 1, n % 4)
            if 20 in slots:
                spread_key_norms()
            for s in range(2 * NBLK):
                if quantise_slot(s) in slots:
                    quantise_q(s)
            for s in range(2 * NBLK):
                if regroup_slot(s) in slots:
                    regroup(s)
            for i in range(NBLK):
                if 8 * i + 16 in slots:
                    norms(i)
            for i in range(1, NBLK - 1):
                if 8 * i + 19 in slots:
                    pair_terms(i)
            for i in due:
                squared_distance(i)
                if i < NBLK - 1:
                    dot_and_cosine(i)
                clamp_distance(i)
                if i < NBLK - 1:
                    row_maxima(i)
            for tau in range(8, 4 * NBLK):
                if input_slot(tau) in slots:
                    input_tile(tau, tau in on_scalar_inputs)

        def shifted_scores(r):
            nc.scalar.activation(out=sq_all[:, r, :], in_=sq_all[:, r, :], func=ACT.Sqrt, scale=w2sq)
            if r % 2 == 0 or r == 7:
                nc.vector.tensor_tensor(out=t_all[:, r, :], in0=t_all[:, r, :], in1=sq_all[:, r, :], op=ALU.subtract)
            else:
                for rt in range(4):
                    c = 4 * r + rt
                    part = slice(LK * rt, LK * (rt + 1))
                    nc.vector.scalar_tensor_tensor(
                        out=t_all[:, r, part], in0=t_all[:, r, part], scalar=negmax[:, c : c + 1],
                        in1=sq_all[:, r, part], op0=ALU.add, op1=ALU.subtract,
                    )

        def softmax_rows(r):
            if r % 2 == 0 or r == 7:
                for rt in range(4):
                    c = 4 * r + rt
                    nc.scalar.activation(
                        out=sq_all[:, r, LK * rt : LK * (rt + 1)], in_=t_all[:, r, LK * rt : LK * (rt + 1)],
                        func=ACT.Exp, bias=negmax[:, c : c + 1], scale=1.0, accum_out=esum[:, c : c + 1],
                    )
            else:
                nc.scalar.activation(out=sq_all[:, r, :], in_=t_all[:, r, :], func=ACT.Exp)

        def row_sums(r):
            if not (r % 2 == 0 or r == 7):
                e3 = sq_all[:, r, :].rearrange("p (t j) -> p t j", t=4)
                nc.vector.tensor_reduce(out=esum[:, 4 * r : 4 * r + 4], in_=e3, axis=AX.X, op=ALU.add)

        def reciprocal_sums(r, tiles):
            c = slice(4 * r + tiles.start, 4 * r + tiles.stop)
            nc.vector.reciprocal(out=rsum[:, c], in_=esum[:, c])

        def normalise(r, tiles):
            e3 = sq_all[:, r, :].rearrange("p (t j) -> p t j", t=4)
            for rt in range(tiles.start, tiles.stop):
                nc.vector.tensor_scalar(
                    out=e3[:, rt, :], in0=e3[:, rt, :], scalar1=rsum[:, 4 * r + rt : 4 * r + rt + 1], scalar2=None,
                    op0=ALU.mult,
                )
            nc.sync.dma_start(out=out_blocks[r][:, tiles.start : tiles.stop, :], in_=e3[:, tiles.start : tiles.stop, :])

        whole = range(0, 4)
        for r in range(8):
            shifted_scores(r)
            if r == 3:
                pair_terms(8)
                dot_and_cosine(8)
                row_maxima(8)
        for r in range(8):
            softmax_rows(r)
            row_sums(r)
            if r > 0:
                normalise(r - 1, whole)
            if r < 7:
                reciprocal_sums(r, whole)
        for tiles in (range(0, 2), range(2, 4)):
            reciprocal_sums(7, tiles)
            normalise(7, tiles)
